import numpy as np
import ml_dtypes


def mxq(x, axis, fmt="e4m3"):
    dtype, down = {"e4m3": (ml_dtypes.float8_e4m3fn, 7), "e5m2": (ml_dtypes.float8_e5m2, 14)}[fmt]
    v = np.moveaxis(np.asarray(x, np.float32).astype(ml_dtypes.bfloat16).astype(np.float64), axis, -1)
    blocks = v.reshape(v.shape[:-1] + (-1, 32))
    amax = np.abs(blocks).max(-1, keepdims=True)
    byte = np.maximum(np.where(amax > 0, np.frexp(amax)[1] - 1 + 127, 0) - down, 1)
    scale = np.exp2(byte - 127.0)
    codes = (blocks / scale).astype(np.float32).astype(dtype).astype(np.float64)
    return np.moveaxis((codes * scale).reshape(v.shape), -1, axis)


WIDE = False


def mx_kscale(k):
    if not WIDE:
        return np.ones(k)
    levels = np.array([10, -10, 5, -5, 0])
    a = np.random.permutation(np.resize(levels, k // 512 * 4)).reshape(k // 512, 4)
    idx = np.arange(k)
    return np.exp2(a[idx // 512, idx % 128 // 32])


BF16 = ml_dtypes.bfloat16


def bf(x):
    return np.asarray(x, np.float32).astype(BF16)


def f64(x):
    return np.asarray(x).astype(np.float64)


E2M1 = np.array([0.0, 0.5, 1.0, 1.5, 2.0, 3.0, 4.0, 6.0, -0.0, -0.5, -1.0, -1.5, -2.0, -3.0, -4.0, -6.0])


def pack_weight(w, fmt):
    k, n = w.shape
    w = f64(bf(w)).reshape(k // 32, 32, n)
    amax = np.abs(w).max(1)
    if fmt == "e4m3":
        byte = np.frexp(amax)[1] - 1 + 127 - 7
    else:
        mant, ex = np.frexp(amax / 6.0)
        byte = np.where(mant > 0.5, ex, ex - 1) + 127
    byte = np.clip(np.where(amax > 0, byte, 1), 1, 254)
    scaled = (w * np.exp2(127.0 - byte)[:, None, :]).reshape(k, n).astype(np.float32)
    by_word = np.ascontiguousarray(scaled.reshape(k // 512, 128, 4, n).transpose(0, 1, 3, 2))
    if fmt == "e4m3":
        words = by_word.astype(ml_dtypes.float8_e4m3fn).view(np.uint8)
    else:
        c = by_word.astype(ml_dtypes.float4_e2m1fn).view(np.uint8) & 0xF
        words = c[..., 0::2] | (c[..., 1::2] << 4)
    return np.ascontiguousarray(words), np.ascontiguousarray(byte.astype(np.uint8).reshape(k // 512, 16, n))


def unpack_weight(words, scales, fmt):
    g, p, n, _ = words.shape
    if fmt == "e4m3":
        vals = np.ascontiguousarray(words).view(ml_dtypes.float8_e4m3fn).astype(np.float64)
    else:
        nib = np.empty((g, p, n, 4), np.uint8)
        nib[..., 0::2] = words & 0xF
        nib[..., 1::2] = words >> 4
        vals = E2M1[nib]
    vals = vals * np.repeat(np.exp2(scales.astype(np.float64) - 127.0), 8, axis=1)[..., None]
    return vals.transpose(0, 1, 3, 2).reshape(g * 512, n)


B, S, D, N = 128, 4, 16384, 256
EPS = 1e-5
FMT = "e4m3"


def batch_bn(x, g, b):
    m = x.mean(axis=0)
    v = x.var(axis=0)
    return g * (x - m) / np.sqrt(v + EPS) + b


def setup_inputs():
    t, u = mx_kscale(D), mx_kscale(D)
    s_z2 = bf(np.random.standard_normal((B, S, D)) * 0.6 + np.random.standard_normal(D) * 0.4)
    c_z2 = bf(np.random.standard_normal((B, D)) * 0.6 + np.random.standard_normal(D) * 0.4)
    s_g2 = bf((1.0 + 0.1 * np.random.standard_normal(D)) * t)
    s_be2 = bf(0.1 * np.random.standard_normal(D) * t)
    s_w3 = np.random.standard_normal((N, D)) * np.sqrt(2.0 / D) / t[None, :]
    s_w3_words, s_w3_scales = pack_weight(np.ascontiguousarray(s_w3.T), FMT)
    s_b3 = bf(0.1 * np.random.standard_normal(N))
    c_g2 = bf((1.0 + 0.1 * np.random.standard_normal(D)) * u)
    c_be2 = bf(0.1 * np.random.standard_normal(D) * u)
    c_w3 = np.random.standard_normal((N, D)) * np.sqrt(2.0 / D) / u[None, :]
    c_w3_words, c_w3_scales = pack_weight(np.ascontiguousarray(c_w3.T), FMT)
    c_b3 = bf(0.1 * np.random.standard_normal(N))
    return {"s_z2": s_z2,
            "c_z2": c_z2,
            "s_g2": s_g2,
            "s_be2": s_be2,
            "s_w3_words": s_w3_words,
            "s_w3_scales": s_w3_scales,
            "s_b3": s_b3,
            "c_g2": c_g2,
            "c_be2": c_be2,
            "c_w3_words": c_w3_words,
            "c_w3_scales": c_w3_scales,
            "c_b3": c_b3}


def reference(s_z2, c_z2, s_g2, s_be2, s_w3_words, s_w3_scales, s_b3, c_g2, c_be2, c_w3_words, c_w3_scales, c_b3):
    c_h = np.maximum(batch_bn(f64(c_z2), f64(c_g2), f64(c_be2)), 0.0)
    c_out = (mxq(c_h, 1, "e4m3") @ unpack_weight(c_w3_words, c_w3_scales, FMT)) + f64(c_b3)
    s_h = np.maximum(batch_bn(f64(s_z2), f64(s_g2), f64(s_be2)), 0.0)
    s_p = (mxq(s_h, 2, "e4m3") @ unpack_weight(s_w3_words, s_w3_scales, FMT)) + f64(s_b3)
    s_out = s_p * c_out[:, None, :]
    aggregated_c = s_out.max(axis=1)
    return (s_out, aggregated_c)

@@ -1,0 +1,291 @@
+from contextlib import ExitStack
+
+import concourse.mybir as mybir
+from concourse.masks import make_identity
+
+F32 = mybir.dt.float32
+BF16 = mybir.dt.bfloat16
+I32 = mybir.dt.int32
+U32 = mybir.dt.uint32
+U8 = mybir.dt.uint8
+FP8X4 = mybir.dt.float8_e4m3fn_x4
+ACT = mybir.ActivationFunctionType
+ALU = mybir.AluOpType
+
+P = 128
+PACK = 4
+K_PASS = P * PACK
+D = 16384
+N = 256
+SLICES = 4
+EPS = 1e-5
+
+GROUPS = D // K_PASS
+STREAMS = 1 + SLICES
+ROUND_GROUPS = 4
+BANK_GROUPS = 2
+ROUND_FEATURES = ROUND_GROUPS * PACK
+STREAM_ROUNDS = GROUPS // ROUND_GROUPS
+ROUNDS = STREAMS * STREAM_ROUNDS
+CHUNK_GROUPS = 8
+CHUNK_ROUNDS = CHUNK_GROUPS // ROUND_GROUPS
+STREAM_CHUNKS = GROUPS // CHUNK_GROUPS
+CHUNKS = STREAMS * STREAM_CHUNKS
+X_BUFS = 4
+
+FLOPS = 2 * P * STREAMS * D * N
+
+
+def tile_cgblock_pb_k_kernel(
+    tc,
+    s_z2,
+    c_z2,
+    s_g2,
+    s_be2,
+    s_w3_words,
+    s_w3_scales,
+    s_b3,
+    c_g2,
+    c_be2,
+    c_w3_words,
+    c_w3_scales,
+    c_b3,
+    out_0,
+    out_1,
+):
+    nc = tc.nc
+    with ExitStack() as ctx:
+        const = ctx.enter_context(tc.tile_pool(name="const", bufs=1))
+        x_pool = ctx.enter_context(tc.tile_pool(name="x", bufs=X_BUFS))
+        small = ctx.enter_context(tc.tile_pool(name="small", bufs=3))
+        hidden = ctx.enter_context(tc.tile_pool(name="hidden", bufs=3))
+        packed = ctx.enter_context(tc.tile_pool(name="packed", bufs=2))
+        turned = ctx.enter_context(tc.psum_pool(name="turned", bufs=6))
+        sums = ctx.enter_context(tc.psum_pool(name="sums", bufs=2))
+        ctx.enter_context(tc.manual_schedule())
+
+        ident = const.tile([P, P], F32)
+        make_identity(nc, ident[:])
+        eps = const.tile([P, 1], F32)
+        nc.vector.memset(eps[:], EPS)
+
+        c_words = const.tile([P, GROUPS, N], U32, align_bytes=64)
+        s_words = const.tile([P, GROUPS, N], U32, align_bytes=64)
+        c_scales = const.tile([P, GROUPS, N], U8, align_bytes=64)
+        s_scales = const.tile([P, GROUPS, N], U8, align_bytes=64)
+        nc.vector.memset(c_scales[:].bitcast(I32), 0)
+        nc.vector.memset(s_scales[:].bitcast(I32), 0)
+        w_words = [c_words, s_words]
+        w_scales = [c_scales, s_scales]
+        w_words_dram = [c_w3_words, s_w3_words]
+        w_scales_dram = [c_w3_scales, s_w3_scales]
+
+        c_bias = const.tile([P, N], BF16)
+        s_bias = const.tile([P, N], BF16)
+        c_out = const.tile([P, N], F32)
+        s_out = const.tile([P, SLICES, N], F32)
+        pooled = const.tile([P, N], F32)
+
+        x_tiles = {}
+        turned_tiles = {}
+        stats_tiles = {}
+        std_tiles = {}
+        affine_tiles = {}
+        plane_tiles = {}
+        grouped_tiles = {}
+        packed_tiles = {}
+        sum_tiles = {}
+
+        def load_x(chunk):
+            stream, part = divmod(chunk, STREAM_CHUNKS)
+            cols = slice(part * CHUNK_GROUPS * K_PASS, (part + 1) * CHUNK_GROUPS * K_PASS)
+            x_sb = x_pool.tile([P, CHUNK_GROUPS * K_PASS], BF16)
+            nc.sync.dma_start(out=x_sb[:], in_=c_z2[:, cols] if stream == 0 else s_z2[:, stream - 1, cols])
+            x_tiles[chunk] = x_sb
+
+        def load_weights(chunk):
+            stream, part = divmod(chunk, STREAM_CHUNKS)
+            if part == 0:
+                for quad in range(4):
+                    nc.sync.dma_start(
+                        out=w_scales[stream][32 * quad : 32 * quad + 4, :, :].bitcast(I32),
+                        in_=w_scales_dram[stream][:, 4 * quad : 4 * quad + 4, :]
+                        .rearrange("g r n -> r g n")
+                        .bitcast(I32),
+                    )
+            groups = slice(part * CHUNK_GROUPS, (part + 1) * CHUNK_GROUPS)
+            nc.sync.dma_start(
+                out=w_words[stream][:, groups, :].bitcast(I32),
+                in_=w_words_dram[stream][groups].rearrange("g p n t -> p g (n t)").bitcast(I32),
+            )
+
+        def transpose_round(r):
+            words = x_tiles[r // CHUNK_ROUNDS][:].bitcast(F32)
+            first = (r % CHUNK_ROUNDS) * ROUND_GROUPS
+            banks = []
+            for half in range(ROUND_GROUPS // BANK_GROUPS):
+                bank = turned.tile([P, 2 * BANK_GROUPS, P], F32)
+                for j in range(2 * BANK_GROUPS):
+                    g = first + half * BANK_GROUPS + j // 2
+                    u = j % 2
+                    nc.tensor.transpose(
+                        bank[:, j, :], words[:, 2 * P * g + u : 2 * P * (g + 1) : 2], ident[:]
+                    )
+                banks.append(bank)
+            turned_tiles[r] = banks
+
+        def pairs_of(r, unit):
+            return turned_tiles[r][unit // 4][:, unit % 4, :].bitcast(BF16)
+
+        def stats_round(r):
+            stats = small.tile([P, 2 * ROUND_GROUPS, 6], F32)
+            for unit in range(2 * ROUND_GROUPS):
+                nc.vector.bn_stats(out=stats[:, unit, :], in_=pairs_of(r, unit))
+            stats_tiles[r] = stats
+
+        def std_round(r):
+            by_feature = stats_tiles[r][:].rearrange("p n (e s) -> p (n e) s", s=3)
+            std = small.tile([P, ROUND_FEATURES], F32)
+            nc.scalar.activation(out=std[:], in_=by_feature[:, :, 2], func=ACT.Sqrt, bias=eps[:], scale=1.0 / P)
+            std_tiles[r] = std
+
+        def affine_round(r):
+            stream, q = divmod(r, STREAM_ROUNDS)
+            gain_row = (2 * GROUPS if stream == 0 else 0) + q * ROUND_GROUPS
+            shift_row = gain_row + GROUPS
+            gain = gain_shift[:, gain_row : gain_row + ROUND_GROUPS, :, :].rearrange("p g u e -> p (g u e)")
+            shift = gain_shift[:, shift_row : shift_row + ROUND_GROUPS, :, :].rearrange("p g u e -> p (g u e)")
+            mean = stats_tiles[r][:].rearrange("p n (e s) -> p (n e) s", s=3)[:, :, 1]
+            rstd = small.tile([P, ROUND_FEATURES], F32)
+            scale = small.tile([P, ROUND_FEATURES], F32)
+            moved = small.tile([P, ROUND_FEATURES], F32)
+            bias = small.tile([P, ROUND_FEATURES], F32)
+            nc.vector.reciprocal(out=rstd[:], in_=std_tiles[r][:])
+            nc.vector.tensor_mul(out=scale[:], in0=rstd[:], in1=gain)
+            nc.vector.scalar_tensor_tensor(
+                out=moved[:], in0=mean, scalar=-1.0, in1=scale[:], op0=ALU.mult, op1=ALU.mult
+            )
+            nc.vector.tensor_add(out=bias[:], in0=moved[:], in1=shift)
+            affine_tiles[r] = (scale, bias)
+
+        def normalise_round(r):
+            scale, bias = affine_tiles[r]
+            planes = hidden.tile([P, ROUND_FEATURES, P], BF16)
+            for unit in range(2 * ROUND_GROUPS):
+                pairs = pairs_of(r, unit).rearrange("p (b e) -> p b e", e=2)
+                for e in range(2):
+                    f = 2 * unit + e
+                    nc.scalar.activation(
+                        out=planes[:, f, :],
+                        in_=pairs[:, :, e],
+                        func=ACT.Relu,
+                        bias=bias[:, f : f + 1],
+                        scale=scale[:, f : f + 1],
+                    )
+            plane_tiles[r] = planes
+
+        def regroup_round(r):
+            grouped = hidden.tile([P, ROUND_GROUPS, P, PACK], BF16, align_bytes=64)
+            nc.gpsimd.tensor_scalar(
+                out=grouped[:],
+                in0=plane_tiles[r][:].rearrange("p (g t) b -> p g b t", t=PACK),
+                scalar1=1.0,
+                scalar2=0.0,
+                op0=ALU.mult,
+                op1=ALU.add,
+            )
+            grouped_tiles[r] = grouped
+
+        def quantise_round(r):
+            codes = packed.tile([P, ROUND_GROUPS * P], U32, align_bytes=64)
+            scales = packed.tile([P, ROUND_GROUPS * P], U8, align_bytes=64)
+            nc.vector.quantize_mx(
+                out=codes[:].bitcast(FP8X4),
+                scales=scales[:],
+                in_=grouped_tiles[r][:].rearrange("p g b t -> p (g b t)"),
+            )
+            packed_tiles[r] = (codes, scales)
+
+        def multiply_round(r):
+            stream, q = divmod(r, STREAM_ROUNDS)
+            which = min(stream, 1)
+            if q == 0:
+                acc = sums.tile([P, N], F32)
+                sum_tiles[stream] = acc
+            codes, scales = packed_tiles[r]
+            for j in range(ROUND_GROUPS):
+                g = q * ROUND_GROUPS + j
+                rows = slice(j * P, (j + 1) * P)
+                nc.tensor.matmul_mx(
+                    out=sum_tiles[stream][:],
+                    lhsT=codes[:, rows].bitcast(FP8X4),
+                    lhsT_scale=scales[:, rows],
+                    rhs=w_words[which][:, g, :].bitcast(FP8X4),
+                    rhs_scale=w_scales[which][:, g, :],
+                    start=(g == 0),
+                    stop=(g == GROUPS - 1),
+                )
+
+        def finish_stream(stream):
+            acc = sum_tiles[stream]
+            if stream == 0:
+                nc.vector.tensor_add(out=c_out[:], in0=acc[:], in1=c_bias[:])
+                return
+            i = stream - 1
+            nc.vector.tensor_add(out=s_out[:, i, :], in0=acc[:], in1=s_bias[:])
+            nc.vector.tensor_mul(out=s_out[:, i, :], in0=s_out[:, i, :], in1=c_out[:])
+            nc.sync.dma_start(out=out_0[:, i, :], in_=s_out[:, i, :])
+            if i == 1:
+                nc.vector.tensor_max(out=pooled[:], in0=s_out[:, 0, :], in1=s_out[:, 1, :])
+            if i > 1:
+                nc.vector.tensor_max(out=pooled[:], in0=pooled[:], in1=s_out[:, i, :])
+            if i == SLICES - 1:
+                nc.sync.dma_start(out=out_1[:], in_=pooled[:])
+
+        load_x(0)
+        vectors = const.tile([P, K_PASS], BF16)
+        for v, vector in enumerate((s_g2, s_be2, c_g2, c_be2)):
+            nc.sync.dma_start(
+                out=vectors[v * GROUPS : (v + 1) * GROUPS, :], in_=vector.rearrange("(g k) -> g k", k=K_PASS)
+            )
+        load_weights(0)
+        for chunk in range(1, X_BUFS):
+            load_x(chunk)
+            load_weights(chunk)
+        nc.sync.dma_start(out=c_bias[:], in_=c_b3.partition_broadcast(P))
+        nc.sync.dma_start(out=s_bias[:], in_=s_b3.partition_broadcast(P))
+
+        transpose_round(0)
+        vectors_t = turned.tile([P, 2 * BANK_GROUPS, P], F32, tag="bank")
+        gain_shift = const.tile([P, P, 2, 2], F32)
+        for u in range(2):
+            nc.tensor.transpose(vectors_t[:, u, :], vectors[:].bitcast(F32)[:, u : 2 * P : 2], ident[:])
+
+        for step in range(ROUNDS + 4):
+            ahead = step + 1
+            if ahead < ROUNDS:
+                transpose_round(ahead)
+                chunk = ahead // CHUNK_ROUNDS + X_BUFS
+                if ahead % CHUNK_ROUNDS == CHUNK_ROUNDS - 1 and chunk < CHUNKS:
+                    load_x(chunk)
+                    if chunk < 2 * STREAM_CHUNKS:
+                        load_weights(chunk)
+            if step < ROUNDS:
+                stats_round(step)
+                std_round(step)
+            if step == 0:
+                for u in range(2):
+                    nc.vector.tensor_copy(
+                        out=gain_shift[:, :, u, :],
+                        in_=vectors_t[:, u, :].bitcast(BF16).rearrange("p (r e) -> p r e", e=2),
+                    )
+            if 0 <= step - 3 < ROUNDS:
+                quantise_round(step - 3)
+                multiply_round(step - 3)
+            if step - 4 >= 0 and (step - 4) % STREAM_ROUNDS == STREAM_ROUNDS - 1:
+                finish_stream((step - 4) // STREAM_ROUNDS)
+            if step < ROUNDS:
+                affine_round(step)
+            if 0 <= step - 1 < ROUNDS:
+                normalise_round(step - 1)
+                regroup_round(step - 1)

@@ -24,6 +24,8 @@ GROUPS = D // K_PASS
 STREAMS = 1 + SLICES
 ROUND_GROUPS = 4
 BANK_GROUPS = 2
+BANK_UNITS = 2 * BANK_GROUPS
+ROUND_UNITS = 2 * ROUND_GROUPS
 ROUND_FEATURES = ROUND_GROUPS * PACK
 STREAM_ROUNDS = GROUPS // ROUND_GROUPS
 ROUNDS = STREAMS * STREAM_ROUNDS
@@ -124,8 +126,8 @@ def tile_cgblock_pb_k_kernel(
             first = (r % CHUNK_ROUNDS) * ROUND_GROUPS
             banks = []
             for half in range(ROUND_GROUPS // BANK_GROUPS):
-                bank = turned.tile([P, 2 * BANK_GROUPS, P], F32)
-                for j in range(2 * BANK_GROUPS):
+                bank = turned.tile([P, BANK_UNITS, P], F32)
+                for j in range(BANK_UNITS):
                     g = first + half * BANK_GROUPS + j // 2
                     u = j % 2
                     nc.tensor.transpose(
@@ -135,13 +137,13 @@ def tile_cgblock_pb_k_kernel(
             turned_tiles[r] = banks
 
         def pairs_of(r, unit):
-            return turned_tiles[r][unit // 4][:, unit % 4, :].bitcast(BF16)
+            return turned_tiles[r][unit // BANK_UNITS][:, unit % BANK_UNITS, :].bitcast(BF16)
 
-        def stats_round(r):
-            stats = small.tile([P, 2 * ROUND_GROUPS, 6], F32)
-            for unit in range(2 * ROUND_GROUPS):
-                nc.vector.bn_stats(out=stats[:, unit, :], in_=pairs_of(r, unit))
-            stats_tiles[r] = stats
+        def stats_unit(r, unit):
+            if unit == 0:
+                stats = small.tile([P, ROUND_UNITS, 6], F32)
+                stats_tiles[r] = stats
+            nc.vector.bn_stats(out=stats_tiles[r][:, unit, :], in_=pairs_of(r, unit))
 
         def std_round(r):
             by_feature = stats_tiles[r][:].rearrange("p n (e s) -> p (n e) s", s=3)
@@ -149,29 +151,38 @@ def tile_cgblock_pb_k_kernel(
             nc.scalar.activation(out=std[:], in_=by_feature[:, :, 2], func=ACT.Sqrt, bias=eps[:], scale=1.0 / P)
             std_tiles[r] = std
 
-        def affine_round(r):
+        def affine_part(r, part):
             stream, q = divmod(r, STREAM_ROUNDS)
             gain_row = (2 * GROUPS if stream == 0 else 0) + q * ROUND_GROUPS
             shift_row = gain_row + GROUPS
             gain = gain_shift[:, gain_row : gain_row + ROUND_GROUPS, :, :].rearrange("p g u e -> p (g u e)")
             shift = gain_shift[:, shift_row : shift_row + ROUND_GROUPS, :, :].rearrange("p g u e -> p (g u e)")
             mean = stats_tiles[r][:].rearrange("p n (e s) -> p (n e) s", s=3)[:, :, 1]
-            rstd = small.tile([P, ROUND_FEATURES], F32)
-            scale = small.tile([P, ROUND_FEATURES], F32)
-            moved = small.tile([P, ROUND_FEATURES], F32)
-            bias = small.tile([P, ROUND_FEATURES], F32)
-            nc.vector.reciprocal(out=rstd[:], in_=std_tiles[r][:])
-            nc.vector.tensor_mul(out=scale[:], in0=rstd[:], in1=gain)
-            nc.vector.scalar_tensor_tensor(
-                out=moved[:], in0=mean, scalar=-1.0, in1=scale[:], op0=ALU.mult, op1=ALU.mult
-            )
-            nc.vector.tensor_add(out=bias[:], in0=moved[:], in1=shift)
-            affine_tiles[r] = (scale, bias)
+            if part == 0:
+                rstd = small.tile([P, ROUND_FEATURES], F32)
+                scale = small.tile([P, ROUND_FEATURES], F32)
+                moved = small.tile([P, ROUND_FEATURES], F32)
+                bias = small.tile([P, ROUND_FEATURES], F32)
+                affine_tiles[r] = (rstd, scale, moved, bias)
+            rstd, scale, moved, bias = affine_tiles[r]
+            if part == 0:
+                nc.vector.reciprocal(out=rstd[:], in_=std_tiles[r][:])
+            if part == 1:
+                nc.vector.tensor_mul(out=scale[:], in0=rstd[:], in1=gain)
+            if part == 2:
+                nc.vector.scalar_tensor_tensor(
+                    out=moved[:], in0=mean, scalar=-1.0, in1=scale[:], op0=ALU.mult, op1=ALU.mult
+                )
+            if part == 3:
+                nc.vector.tensor_add(out=bias[:], in0=moved[:], in1=shift)
 
-        def normalise_round(r):
-            scale, bias = affine_tiles[r]
-            planes = hidden.tile([P, ROUND_FEATURES, P], BF16)
-            for unit in range(2 * ROUND_GROUPS):
+        def normalise_bank(r, half):
+            rstd, scale, moved, bias = affine_tiles[r]
+            if half == 0:
+                planes = hidden.tile([P, ROUND_FEATURES, P], BF16)
+                plane_tiles[r] = planes
+            planes = plane_tiles[r]
+            for unit in range(half * BANK_UNITS, (half + 1) * BANK_UNITS):
                 pairs = pairs_of(r, unit).rearrange("p (b e) -> p b e", e=2)
                 for e in range(2):
                     f = 2 * unit + e
@@ -182,7 +193,6 @@ def tile_cgblock_pb_k_kernel(
                         bias=bias[:, f : f + 1],
                         scale=scale[:, f : f + 1],
                     )
-            plane_tiles[r] = planes
 
         def regroup_round(r):
             grouped = hidden.tile([P, ROUND_GROUPS, P, PACK], BF16, align_bytes=64)
@@ -256,36 +266,44 @@ def tile_cgblock_pb_k_kernel(
         nc.sync.dma_start(out=s_bias[:], in_=s_b3.partition_broadcast(P))
 
         transpose_round(0)
-        vectors_t = turned.tile([P, 2 * BANK_GROUPS, P], F32, tag="bank")
+        vectors_t = turned.tile([P, BANK_UNITS, P], F32, tag="bank")
         gain_shift = const.tile([P, P, 2, 2], F32)
         for u in range(2):
             nc.tensor.transpose(vectors_t[:, u, :], vectors[:].bitcast(F32)[:, u : 2 * P : 2], ident[:])
 
+        def live(r):
+            return 0 <= r < ROUNDS
+
         for step in range(ROUNDS + 4):
+            if live(step - 1):
+                std_round(step - 1)
+            if live(step - 2):
+                normalise_bank(step - 2, 1)
+                regroup_round(step - 2)
             ahead = step + 1
-            if ahead < ROUNDS:
+            if live(ahead):
                 transpose_round(ahead)
                 chunk = ahead // CHUNK_ROUNDS + X_BUFS
                 if ahead % CHUNK_ROUNDS == CHUNK_ROUNDS - 1 and chunk < CHUNKS:
                     load_x(chunk)
                     if chunk < 2 * STREAM_CHUNKS:
                         load_weights(chunk)
-            if step < ROUNDS:
-                stats_round(step)
-                std_round(step)
+            for unit in range(ROUND_UNITS):
+                if live(step):
+                    stats_unit(step, unit)
+                if unit < 4 and live(step - 1):
+                    affine_part(step - 1, unit)
+                if unit == 5 and live(step - 3):
+                    quantise_round(step - 3)
             if step == 0:
                 for u in range(2):
                     nc.vector.tensor_copy(
                         out=gain_shift[:, :, u, :],
                         in_=vectors_t[:, u, :].bitcast(BF16).rearrange("p (r e) -> p r e", e=2),
                     )
-            if 0 <= step - 3 < ROUNDS:
-                quantise_round(step - 3)
+            if live(step - 3):
                 multiply_round(step - 3)
             if step - 4 >= 0 and (step - 4) % STREAM_ROUNDS == STREAM_ROUNDS - 1:
                 finish_stream((step - 4) // STREAM_ROUNDS)
-            if step < ROUNDS:
-                affine_round(step)
-            if 0 <= step - 1 < ROUNDS:
-                normalise_round(step - 1)
-                regroup_round(step - 1)
+            if live(step - 1):
+                normalise_bank(step - 1, 0)

@@ -34,6 +34,7 @@ CHUNK_ROUNDS = CHUNK_GROUPS // ROUND_GROUPS
 STREAM_CHUNKS = GROUPS // CHUNK_GROUPS
 CHUNKS = STREAMS * STREAM_CHUNKS
 X_BUFS = 4
+RUN = 4
 
 FLOPS = 2 * P * STREAMS * D * N
 
@@ -194,17 +195,14 @@ def tile_cgblock_pb_k_kernel(
                         scale=scale[:, f : f + 1],
                     )
 
-        def regroup_round(r):
-            grouped = hidden.tile([P, ROUND_GROUPS, P, PACK], BF16, align_bytes=64)
-            nc.gpsimd.tensor_scalar(
-                out=grouped[:],
-                in0=plane_tiles[r][:].rearrange("p (g t) b -> p g b t", t=PACK),
-                scalar1=1.0,
-                scalar2=0.0,
-                op0=ALU.mult,
-                op1=ALU.add,
+        def regroup_group(r, j):
+            if j == 0:
+                grouped = hidden.tile([P, ROUND_GROUPS, P, PACK], BF16, align_bytes=64)
+                grouped_tiles[r] = grouped
+            nc.vector.tensor_copy(
+                out=grouped_tiles[r][:, j, :, :].rearrange("p (c i) t -> p c t i", i=RUN),
+                in_=plane_tiles[r][:, j * PACK : (j + 1) * PACK, :].rearrange("p t (c i) -> p c t i", i=RUN),
             )
-            grouped_tiles[r] = grouped
 
         def quantise_round(r):
             codes = packed.tile([P, ROUND_GROUPS * P], U32, align_bytes=64)
@@ -279,7 +277,6 @@ def tile_cgblock_pb_k_kernel(
                 std_round(step - 1)
             if live(step - 2):
                 normalise_bank(step - 2, 1)
-                regroup_round(step - 2)
             ahead = step + 1
             if live(ahead):
                 transpose_round(ahead)
@@ -295,6 +292,8 @@ def tile_cgblock_pb_k_kernel(
                     affine_part(step - 1, unit)
                 if unit == 5 and live(step - 3):
                     quantise_round(step - 3)
+                if unit >= 4 and live(step - 2):
+                    regroup_group(step - 2, unit - 4)
             if step == 0:
                 for u in range(2):
                     nc.vector.tensor_copy(

@@ -29,12 +29,13 @@ ROUND_UNITS = 2 * ROUND_GROUPS
 ROUND_FEATURES = ROUND_GROUPS * PACK
 STREAM_ROUNDS = GROUPS // ROUND_GROUPS
 ROUNDS = STREAMS * STREAM_ROUNDS
-CHUNK_GROUPS = 8
+CHUNK_GROUPS = 4
 CHUNK_ROUNDS = CHUNK_GROUPS // ROUND_GROUPS
 STREAM_CHUNKS = GROUPS // CHUNK_GROUPS
 CHUNKS = STREAMS * STREAM_CHUNKS
-X_BUFS = 4
+X_BUFS = 8
 RUN = 4
+SCALAR_GROUPS = 2
 
 FLOPS = 2 * P * STREAMS * D * N
 
@@ -136,6 +137,11 @@ def tile_cgblock_pb_k_kernel(
                     )
                 banks.append(bank)
             turned_tiles[r] = banks
+            chunk = r // CHUNK_ROUNDS + X_BUFS
+            if r % CHUNK_ROUNDS == CHUNK_ROUNDS - 1 and chunk < CHUNKS:
+                load_x(chunk)
+                if chunk < 2 * STREAM_CHUNKS:
+                    load_weights(chunk)
 
         def pairs_of(r, unit):
             return turned_tiles[r][unit // BANK_UNITS][:, unit % BANK_UNITS, :].bitcast(BF16)
@@ -195,14 +201,19 @@ def tile_cgblock_pb_k_kernel(
                         scale=scale[:, f : f + 1],
                     )
 
+        def scalar_share(r):
+            return SCALAR_GROUPS if r < ROUNDS - 2 else 0
+
         def regroup_group(r, j):
             if j == 0:
                 grouped = hidden.tile([P, ROUND_GROUPS, P, PACK], BF16, align_bytes=64)
                 grouped_tiles[r] = grouped
-            nc.vector.tensor_copy(
-                out=grouped_tiles[r][:, j, :, :].rearrange("p (c i) t -> p c t i", i=RUN),
-                in_=plane_tiles[r][:, j * PACK : (j + 1) * PACK, :].rearrange("p t (c i) -> p c t i", i=RUN),
-            )
+            words = grouped_tiles[r][:, j, :, :].rearrange("p (c i) t -> p c t i", i=RUN)
+            planes = plane_tiles[r][:, j * PACK : (j + 1) * PACK, :].rearrange("p t (c i) -> p c t i", i=RUN)
+            if j < scalar_share(r):
+                nc.scalar.copy(out=words, in_=planes)
+            else:
+                nc.vector.tensor_copy(out=words, in_=planes)
 
         def quantise_round(r):
             codes = packed.tile([P, ROUND_GROUPS * P], U32, align_bytes=64)
@@ -248,7 +259,7 @@ def tile_cgblock_pb_k_kernel(
             if i > 1:
                 nc.vector.tensor_max(out=pooled[:], in0=pooled[:], in1=s_out[:, i, :])
             if i == SLICES - 1:
-                nc.sync.dma_start(out=out_1[:], in_=pooled[:])
+                nc.scalar.dma_start(out=out_1[:], in_=pooled[:])
 
         load_x(0)
         vectors = const.tile([P, K_PASS], BF16)
@@ -276,15 +287,12 @@ def tile_cgblock_pb_k_kernel(
             if live(step - 1):
                 std_round(step - 1)
             if live(step - 2):
+                for j in range(scalar_share(step - 2)):
+                    regroup_group(step - 2, j)
                 normalise_bank(step - 2, 1)
             ahead = step + 1
             if live(ahead):
                 transpose_round(ahead)
-                chunk = ahead // CHUNK_ROUNDS + X_BUFS
-                if ahead % CHUNK_ROUNDS == CHUNK_ROUNDS - 1 and chunk < CHUNKS:
-                    load_x(chunk)
-                    if chunk < 2 * STREAM_CHUNKS:
-                        load_weights(chunk)
             for unit in range(ROUND_UNITS):
                 if live(step):
                     stats_unit(step, unit)
@@ -292,7 +300,7 @@ def tile_cgblock_pb_k_kernel(
                     affine_part(step - 1, unit)
                 if unit == 5 and live(step - 3):
                     quantise_round(step - 3)
-                if unit >= 4 and live(step - 2):
+                if live(step - 2) and unit - 4 >= scalar_share(step - 2):
                     regroup_group(step - 2, unit - 4)
             if step == 0:
                 for u in range(2):

@@ -35,7 +35,7 @@ STREAM_CHUNKS = GROUPS // CHUNK_GROUPS
 CHUNKS = STREAMS * STREAM_CHUNKS
 X_BUFS = 8
 RUN = 4
-SCALAR_GROUPS = 2
+SCALAR_GROUPS = 1
 
 FLOPS = 2 * P * STREAMS * D * N
 
@@ -181,7 +181,7 @@ def tile_cgblock_pb_k_kernel(
                     out=moved[:], in0=mean, scalar=-1.0, in1=scale[:], op0=ALU.mult, op1=ALU.mult
                 )
             if part == 3:
-                nc.vector.tensor_add(out=bias[:], in0=moved[:], in1=shift)
+                nc.gpsimd.tensor_tensor(out=bias[:], in0=moved[:], in1=shift, op=ALU.add)
 
         def normalise_bank(r, half):
             rstd, scale, moved, bias = affine_tiles[r]
@@ -201,19 +201,27 @@ def tile_cgblock_pb_k_kernel(
                         scale=scale[:, f : f + 1],
                     )
 
-        def scalar_share(r):
-            return SCALAR_GROUPS if r < ROUNDS - 2 else 0
-
         def regroup_group(r, j):
             if j == 0:
                 grouped = hidden.tile([P, ROUND_GROUPS, P, PACK], BF16, align_bytes=64)
                 grouped_tiles[r] = grouped
-            words = grouped_tiles[r][:, j, :, :].rearrange("p (c i) t -> p c t i", i=RUN)
-            planes = plane_tiles[r][:, j * PACK : (j + 1) * PACK, :].rearrange("p t (c i) -> p c t i", i=RUN)
-            if j < scalar_share(r):
-                nc.scalar.copy(out=words, in_=planes)
+            words = grouped_tiles[r][:, j, :, :]
+            planes = plane_tiles[r][:, j * PACK : (j + 1) * PACK, :]
+            word_runs = words.rearrange("p (c i) t -> p c t i", i=RUN)
+            plane_runs = planes.rearrange("p t (c i) -> p c t i", i=RUN)
+            if r >= ROUNDS - 2:
+                nc.vector.tensor_copy(out=word_runs, in_=plane_runs)
+            elif j < SCALAR_GROUPS:
+                nc.scalar.copy(out=word_runs, in_=plane_runs)
             else:
-                nc.vector.tensor_copy(out=words, in_=planes)
+                nc.gpsimd.tensor_scalar(
+                    out=words,
+                    in0=planes.rearrange("p t b -> p b t"),
+                    scalar1=1.0,
+                    scalar2=0.0,
+                    op0=ALU.mult,
+                    op1=ALU.add,
+                )
 
         def quantise_round(r):
             codes = packed.tile([P, ROUND_GROUPS * P], U32, align_bytes=64)
@@ -284,11 +292,13 @@ def tile_cgblock_pb_k_kernel(
             return 0 <= r < ROUNDS
 
         for step in range(ROUNDS + 4):
+            last_rounds = step - 2 >= ROUNDS - 2
             if live(step - 1):
                 std_round(step - 1)
             if live(step - 2):
-                for j in range(scalar_share(step - 2)):
-                    regroup_group(step - 2, j)
+                if not last_rounds:
+                    for j in range(SCALAR_GROUPS):
+                        regroup_group(step - 2, j)
                 normalise_bank(step - 2, 1)
             ahead = step + 1
             if live(ahead):
@@ -296,12 +306,20 @@ def tile_cgblock_pb_k_kernel(
             for unit in range(ROUND_UNITS):
                 if live(step):
                     stats_unit(step, unit)
-                if unit < 4 and live(step - 1):
-                    affine_part(step - 1, unit)
-                if unit == 5 and live(step - 3):
-                    quantise_round(step - 3)
-                if live(step - 2) and unit - 4 >= scalar_share(step - 2):
-                    regroup_group(step - 2, unit - 4)
+                if unit == 2 and live(step - 1):
+                    affine_part(step - 1, 0)
+                if unit == 3:
+                    if live(step - 1):
+                        affine_part(step - 1, 1)
+                    if live(step - 3):
+                        quantise_round(step - 3)
+                    if live(step - 1):
+                        affine_part(step - 1, 2)
+            if live(step - 1):
+                affine_part(step - 1, 3)
+            if live(step - 2):
+                for j in range(0 if last_rounds else SCALAR_GROUPS, ROUND_GROUPS):
+                    regroup_group(step - 2, j)
             if step == 0:
                 for u in range(2):
                     nc.vector.tensor_copy(

@@ -201,27 +201,23 @@ def tile_cgblock_pb_k_kernel(
                         scale=scale[:, f : f + 1],
                     )
 
-        def regroup_group(r, j):
+        def regroup_by_copy(r, j, copy):
             if j == 0:
                 grouped = hidden.tile([P, ROUND_GROUPS, P, PACK], BF16, align_bytes=64)
                 grouped_tiles[r] = grouped
-            words = grouped_tiles[r][:, j, :, :]
-            planes = plane_tiles[r][:, j * PACK : (j + 1) * PACK, :]
-            word_runs = words.rearrange("p (c i) t -> p c t i", i=RUN)
-            plane_runs = planes.rearrange("p t (c i) -> p c t i", i=RUN)
-            if r >= ROUNDS - 2:
-                nc.vector.tensor_copy(out=word_runs, in_=plane_runs)
-            elif j < SCALAR_GROUPS:
-                nc.scalar.copy(out=word_runs, in_=plane_runs)
-            else:
-                nc.gpsimd.tensor_scalar(
-                    out=words,
-                    in0=planes.rearrange("p t b -> p b t"),
-                    scalar1=1.0,
-                    scalar2=0.0,
-                    op0=ALU.mult,
-                    op1=ALU.add,
-                )
+            words = grouped_tiles[r][:, j, :, :].rearrange("p (c i) t -> p c t i", i=RUN)
+            planes = plane_tiles[r][:, j * PACK : (j + 1) * PACK, :].rearrange("p t (c i) -> p c t i", i=RUN)
+            copy(out=words, in_=planes)
+
+        def regroup_on_gpsimd(r):
+            nc.gpsimd.tensor_scalar(
+                out=grouped_tiles[r][:, SCALAR_GROUPS:, :, :],
+                in0=plane_tiles[r][:, SCALAR_GROUPS * PACK :, :].rearrange("p (g t) b -> p g b t", t=PACK),
+                scalar1=1.0,
+                scalar2=0.0,
+                op0=ALU.mult,
+                op1=ALU.add,
+            )
 
         def quantise_round(r):
             codes = packed.tile([P, ROUND_GROUPS * P], U32, align_bytes=64)
@@ -298,7 +294,7 @@ def tile_cgblock_pb_k_kernel(
             if live(step - 2):
                 if not last_rounds:
                     for j in range(SCALAR_GROUPS):
-                        regroup_group(step - 2, j)
+                        regroup_by_copy(step - 2, j, nc.scalar.copy)
                 normalise_bank(step - 2, 1)
             ahead = step + 1
             if live(ahead):
@@ -318,8 +314,11 @@ def tile_cgblock_pb_k_kernel(
             if live(step - 1):
                 affine_part(step - 1, 3)
             if live(step - 2):
-                for j in range(0 if last_rounds else SCALAR_GROUPS, ROUND_GROUPS):
-                    regroup_group(step - 2, j)
+                if last_rounds:
+                    for j in range(ROUND_GROUPS):
+                        regroup_by_copy(step - 2, j, nc.vector.tensor_copy)
+                else:
+                    regroup_on_gpsimd(step - 2)
             if step == 0:
                 for u in range(2):
                     nc.vector.tensor_copy(

@@ -35,7 +35,7 @@ STREAM_CHUNKS = GROUPS // CHUNK_GROUPS
 CHUNKS = STREAMS * STREAM_CHUNKS
 X_BUFS = 8
 RUN = 4
-SCALAR_GROUPS = 1
+GPSIMD_GROUPS = ROUND_GROUPS - 1
 
 FLOPS = 2 * P * STREAMS * D * N
 
@@ -63,6 +63,8 @@ def tile_cgblock_pb_k_kernel(
         x_pool = ctx.enter_context(tc.tile_pool(name="x", bufs=X_BUFS))
         small = ctx.enter_context(tc.tile_pool(name="small", bufs=3))
         hidden = ctx.enter_context(tc.tile_pool(name="hidden", bufs=3))
+        gpsimd_words = ctx.enter_context(tc.tile_pool(name="gpsimd_words", bufs=1))
+        scalar_words = ctx.enter_context(tc.tile_pool(name="scalar_words", bufs=2))
         packed = ctx.enter_context(tc.tile_pool(name="packed", bufs=2))
         turned = ctx.enter_context(tc.psum_pool(name="turned", bufs=6))
         sums = ctx.enter_context(tc.psum_pool(name="sums", bufs=2))
@@ -147,7 +149,7 @@ def tile_cgblock_pb_k_kernel(
             return turned_tiles[r][unit // BANK_UNITS][:, unit % BANK_UNITS, :].bitcast(BF16)
 
         def stats_unit(r, unit):
-            if unit == 0:
+            if r not in stats_tiles:
                 stats = small.tile([P, ROUND_UNITS, 6], F32)
                 stats_tiles[r] = stats
             nc.vector.bn_stats(out=stats_tiles[r][:, unit, :], in_=pairs_of(r, unit))
@@ -181,7 +183,7 @@ def tile_cgblock_pb_k_kernel(
                     out=moved[:], in0=mean, scalar=-1.0, in1=scale[:], op0=ALU.mult, op1=ALU.mult
                 )
             if part == 3:
-                nc.gpsimd.tensor_tensor(out=bias[:], in0=moved[:], in1=shift, op=ALU.add)
+                nc.vector.tensor_add(out=bias[:], in0=moved[:], in1=shift)
 
         def normalise_bank(r, half):
             rstd, scale, moved, bias = affine_tiles[r]
@@ -201,33 +203,51 @@ def tile_cgblock_pb_k_kernel(
                         scale=scale[:, f : f + 1],
                     )
 
-        def regroup_by_copy(r, j, copy):
-            if j == 0:
-                grouped = hidden.tile([P, ROUND_GROUPS, P, PACK], BF16, align_bytes=64)
-                grouped_tiles[r] = grouped
-            words = grouped_tiles[r][:, j, :, :].rearrange("p (c i) t -> p c t i", i=RUN)
-            planes = plane_tiles[r][:, j * PACK : (j + 1) * PACK, :].rearrange("p t (c i) -> p c t i", i=RUN)
-            copy(out=words, in_=planes)
+        def words_of(r):
+            if r not in grouped_tiles:
+                by_scalar = scalar_words.tile([P, 1, P, PACK], BF16, align_bytes=64)
+                by_gpsimd = gpsimd_words.tile([P, GPSIMD_GROUPS, P, PACK], BF16, align_bytes=64)
+                grouped_tiles[r] = (by_scalar, by_gpsimd)
+            return grouped_tiles[r]
+
+        def regroup_by_copy(words, r, j, copy):
+            planes = plane_tiles[r][:, j * PACK : (j + 1) * PACK, :]
+            copy(
+                out=words.rearrange("p (c i) t -> p c t i", i=RUN),
+                in_=planes.rearrange("p t (c i) -> p c t i", i=RUN),
+            )
+
+        def regroup_on_scalar(r):
+            regroup_by_copy(words_of(r)[0][:, 0, :, :], r, 0, nc.scalar.copy)
+
+        def regroup_on_vector(r):
+            for j in range(GPSIMD_GROUPS):
+                regroup_by_copy(words_of(r)[1][:, j, :, :], r, j + 1, nc.vector.tensor_copy)
 
         def regroup_on_gpsimd(r):
             nc.gpsimd.tensor_scalar(
-                out=grouped_tiles[r][:, SCALAR_GROUPS:, :, :],
-                in0=plane_tiles[r][:, SCALAR_GROUPS * PACK :, :].rearrange("p (g t) b -> p g b t", t=PACK),
+                out=words_of(r)[1][:],
+                in0=plane_tiles[r][:, PACK:, :].rearrange("p (g t) b -> p g b t", t=PACK),
                 scalar1=1.0,
                 scalar2=0.0,
                 op0=ALU.mult,
                 op1=ALU.add,
             )
 
-        def quantise_round(r):
-            codes = packed.tile([P, ROUND_GROUPS * P], U32, align_bytes=64)
-            scales = packed.tile([P, ROUND_GROUPS * P], U8, align_bytes=64)
+        def quantise_part(r, first, groups):
+            if r not in packed_tiles:
+                codes = packed.tile([P, ROUND_GROUPS * P], U32, align_bytes=64)
+                scales = packed.tile([P, ROUND_GROUPS * P], U8, align_bytes=64)
+                packed_tiles[r] = (codes, scales)
+            codes, scales = packed_tiles[r]
+            by_scalar, by_gpsimd = words_of(r)
+            words = by_scalar[:] if first == 0 else by_gpsimd[:, first - 1 : first - 1 + groups, :, :]
+            cols = slice(first * P, (first + groups) * P)
             nc.vector.quantize_mx(
-                out=codes[:].bitcast(FP8X4),
-                scales=scales[:],
-                in_=grouped_tiles[r][:].rearrange("p g b t -> p (g b t)"),
+                out=codes[:, cols].bitcast(FP8X4),
+                scales=scales[:, cols],
+                in_=words.rearrange("p g b t -> p (g b t)"),
             )
-            packed_tiles[r] = (codes, scales)
 
         def multiply_round(r):
             stream, q = divmod(r, STREAM_ROUNDS)
@@ -288,35 +308,37 @@ def tile_cgblock_pb_k_kernel(
             return 0 <= r < ROUNDS
 
         for step in range(ROUNDS + 4):
-            last_rounds = step - 2 >= ROUNDS - 2
             if live(step - 1):
                 std_round(step - 1)
             if live(step - 2):
-                if not last_rounds:
-                    for j in range(SCALAR_GROUPS):
-                        regroup_by_copy(step - 2, j, nc.scalar.copy)
+                regroup_on_scalar(step - 2)
                 normalise_bank(step - 2, 1)
             ahead = step + 1
             if live(ahead):
                 transpose_round(ahead)
-            for unit in range(ROUND_UNITS):
+            for unit in range(BANK_UNITS - 1, -1, -1):
                 if live(step):
                     stats_unit(step, unit)
-                if unit == 2 and live(step - 1):
+                if unit == 1 and live(step - 1):
                     affine_part(step - 1, 0)
-                if unit == 3:
-                    if live(step - 1):
-                        affine_part(step - 1, 1)
-                    if live(step - 3):
-                        quantise_round(step - 3)
-                    if live(step - 1):
-                        affine_part(step - 1, 2)
+            if live(step - 1):
+                affine_part(step - 1, 1)
+            if live(step - 3):
+                quantise_part(step - 3, 2, 2)
+            if live(step - 1):
+                affine_part(step - 1, 2)
+            if live(step - 3):
+                quantise_part(step - 3, 0, 1)
             if live(step - 1):
                 affine_part(step - 1, 3)
+            if live(step - 3):
+                quantise_part(step - 3, 1, 1)
+            if live(step):
+                for unit in range(ROUND_UNITS - 1, BANK_UNITS - 1, -1):
+                    stats_unit(step, unit)
             if live(step - 2):
-                if last_rounds:
-                    for j in range(ROUND_GROUPS):
-                        regroup_by_copy(step - 2, j, nc.vector.tensor_copy)
+                if step - 2 >= ROUNDS - 2:
+                    regroup_on_vector(step - 2)
                 else:
                     regroup_on_gpsimd(step - 2)
             if step == 0:

@@ -35,7 +35,8 @@ STREAM_CHUNKS = GROUPS // CHUNK_GROUPS
 CHUNKS = STREAMS * STREAM_CHUNKS
 X_BUFS = 8
 RUN = 4
-GPSIMD_GROUPS = ROUND_GROUPS - 1
+ROUND_COLS = ROUND_GROUPS * P
+SCALAR_COLS = P // 2
 
 FLOPS = 2 * P * STREAMS * D * N
 
@@ -63,8 +64,7 @@ def tile_cgblock_pb_k_kernel(
         x_pool = ctx.enter_context(tc.tile_pool(name="x", bufs=X_BUFS))
         small = ctx.enter_context(tc.tile_pool(name="small", bufs=3))
         hidden = ctx.enter_context(tc.tile_pool(name="hidden", bufs=3))
-        gpsimd_words = ctx.enter_context(tc.tile_pool(name="gpsimd_words", bufs=1))
-        scalar_words = ctx.enter_context(tc.tile_pool(name="scalar_words", bufs=2))
+        regrouped = ctx.enter_context(tc.tile_pool(name="regrouped", bufs=1))
         packed = ctx.enter_context(tc.tile_pool(name="packed", bufs=2))
         turned = ctx.enter_context(tc.psum_pool(name="turned", bufs=6))
         sums = ctx.enter_context(tc.psum_pool(name="sums", bufs=2))
@@ -188,7 +188,7 @@ def tile_cgblock_pb_k_kernel(
         def normalise_bank(r, half):
             rstd, scale, moved, bias = affine_tiles[r]
             if half == 0:
-                planes = hidden.tile([P, ROUND_FEATURES, P], BF16)
+                planes = hidden.tile([P, PACK, ROUND_GROUPS, P], BF16)
                 plane_tiles[r] = planes
             planes = plane_tiles[r]
             for unit in range(half * BANK_UNITS, (half + 1) * BANK_UNITS):
@@ -196,57 +196,48 @@ def tile_cgblock_pb_k_kernel(
                 for e in range(2):
                     f = 2 * unit + e
                     nc.scalar.activation(
-                        out=planes[:, f, :],
+                        out=planes[:, f % PACK, f // PACK, :],
                         in_=pairs[:, :, e],
                         func=ACT.Relu,
                         bias=bias[:, f : f + 1],
                         scale=scale[:, f : f + 1],
                     )
 
-        def words_of(r):
-            if r not in grouped_tiles:
-                by_scalar = scalar_words.tile([P, 1, P, PACK], BF16, align_bytes=64)
-                by_gpsimd = gpsimd_words.tile([P, GPSIMD_GROUPS, P, PACK], BF16, align_bytes=64)
-                grouped_tiles[r] = (by_scalar, by_gpsimd)
-            return grouped_tiles[r]
-
-        def regroup_by_copy(words, r, j, copy):
-            planes = plane_tiles[r][:, j * PACK : (j + 1) * PACK, :]
+        def regroup_by_copy(r, cols, copy):
+            planes = plane_tiles[r][:].rearrange("p t g b -> p t (g b)")[:, :, cols]
             copy(
-                out=words.rearrange("p (c i) t -> p c t i", i=RUN),
+                out=grouped_tiles[r][:, cols, :].rearrange("p (c i) t -> p c t i", i=RUN),
                 in_=planes.rearrange("p t (c i) -> p c t i", i=RUN),
             )
 
-        def regroup_on_scalar(r):
-            regroup_by_copy(words_of(r)[0][:, 0, :, :], r, 0, nc.scalar.copy)
-
-        def regroup_on_vector(r):
-            for j in range(GPSIMD_GROUPS):
-                regroup_by_copy(words_of(r)[1][:, j, :, :], r, j + 1, nc.vector.tensor_copy)
-
-        def regroup_on_gpsimd(r):
+        def regroup_round(r):
+            grouped = regrouped.tile([P, ROUND_COLS, PACK], BF16, align_bytes=64)
+            grouped_tiles[r] = grouped
+            if r >= ROUNDS - 2:
+                regroup_by_copy(r, slice(0, ROUND_COLS), nc.vector.tensor_copy)
+                return
+            regroup_by_copy(r, slice(0, SCALAR_COLS), nc.scalar.copy)
+            planes = plane_tiles[r][:].rearrange("p t g b -> p t (g b)")
             nc.gpsimd.tensor_scalar(
-                out=words_of(r)[1][:],
-                in0=plane_tiles[r][:, PACK:, :].rearrange("p (g t) b -> p g b t", t=PACK),
+                out=grouped[:, SCALAR_COLS:, :],
+                in0=planes[:, :, SCALAR_COLS:].rearrange("p t c -> p c t"),
                 scalar1=1.0,
                 scalar2=0.0,
                 op0=ALU.mult,
                 op1=ALU.add,
             )
 
-        def quantise_part(r, first, groups):
-            if r not in packed_tiles:
-                codes = packed.tile([P, ROUND_GROUPS * P], U32, align_bytes=64)
-                scales = packed.tile([P, ROUND_GROUPS * P], U8, align_bytes=64)
+        def quantise_half(r, half):
+            if half == 0:
+                codes = packed.tile([P, ROUND_COLS], U32, align_bytes=64)
+                scales = packed.tile([P, ROUND_COLS], U8, align_bytes=64)
                 packed_tiles[r] = (codes, scales)
             codes, scales = packed_tiles[r]
-            by_scalar, by_gpsimd = words_of(r)
-            words = by_scalar[:] if first == 0 else by_gpsimd[:, first - 1 : first - 1 + groups, :, :]
-            cols = slice(first * P, (first + groups) * P)
+            cols = slice(half * ROUND_COLS // 2, (half + 1) * ROUND_COLS // 2)
             nc.vector.quantize_mx(
                 out=codes[:, cols].bitcast(FP8X4),
                 scales=scales[:, cols],
-                in_=words.rearrange("p g b t -> p (g b t)"),
+                in_=grouped_tiles[r][:, cols, :].rearrange("p c t -> p (c t)"),
             )
 
         def multiply_round(r):
@@ -311,36 +302,28 @@ def tile_cgblock_pb_k_kernel(
             if live(step - 1):
                 std_round(step - 1)
             if live(step - 2):
-                regroup_on_scalar(step - 2)
                 normalise_bank(step - 2, 1)
             ahead = step + 1
             if live(ahead):
                 transpose_round(ahead)
-            for unit in range(BANK_UNITS - 1, -1, -1):
+            for unit in (3, 2, 1, 0, 7, 6, 5, 4):
                 if live(step):
                     stats_unit(step, unit)
                 if unit == 1 and live(step - 1):
                     affine_part(step - 1, 0)
-            if live(step - 1):
-                affine_part(step - 1, 1)
-            if live(step - 3):
-                quantise_part(step - 3, 2, 2)
-            if live(step - 1):
-                affine_part(step - 1, 2)
-            if live(step - 3):
-                quantise_part(step - 3, 0, 1)
-            if live(step - 1):
-                affine_part(step - 1, 3)
-            if live(step - 3):
-                quantise_part(step - 3, 1, 1)
-            if live(step):
-                for unit in range(ROUND_UNITS - 1, BANK_UNITS - 1, -1):
-                    stats_unit(step, unit)
+                if unit == 0 and live(step - 1):
+                    affine_part(step - 1, 1)
+                if unit == 7:
+                    if live(step - 3):
+                        quantise_half(step - 3, 0)
+                    if live(step - 1):
+                        affine_part(step - 1, 2)
+                    if live(step - 3):
+                        quantise_half(step - 3, 1)
+                    if live(step - 1):
+                        affine_part(step - 1, 3)
             if live(step - 2):
-                if step - 2 >= ROUNDS - 2:
-                    regroup_on_vector(step - 2)
-                else:
-                    regroup_on_gpsimd(step - 2)
+                regroup_round(step - 2)
             if step == 0:
                 for u in range(2):
                     nc.vector.tensor_copy(

@@ -36,7 +36,7 @@ CHUNKS = STREAMS * STREAM_CHUNKS
 X_BUFS = 8
 RUN = 4
 ROUND_COLS = ROUND_GROUPS * P
-SCALAR_COLS = P // 2
+SCALAR_COLS = 3 * P // 4
 
 FLOPS = 2 * P * STREAMS * D * N
 
@@ -64,7 +64,7 @@ def tile_cgblock_pb_k_kernel(
         x_pool = ctx.enter_context(tc.tile_pool(name="x", bufs=X_BUFS))
         small = ctx.enter_context(tc.tile_pool(name="small", bufs=3))
         hidden = ctx.enter_context(tc.tile_pool(name="hidden", bufs=3))
-        regrouped = ctx.enter_context(tc.tile_pool(name="regrouped", bufs=1))
+        regrouped = ctx.enter_context(tc.tile_pool(name="regrouped", bufs=3))
         packed = ctx.enter_context(tc.tile_pool(name="packed", bufs=2))
         turned = ctx.enter_context(tc.psum_pool(name="turned", bufs=6))
         sums = ctx.enter_context(tc.psum_pool(name="sums", bufs=2))
@@ -99,6 +99,7 @@ def tile_cgblock_pb_k_kernel(
         affine_tiles = {}
         plane_tiles = {}
         grouped_tiles = {}
+        zero_tiles = {}
         packed_tiles = {}
         sum_tiles = {}
 
@@ -210,6 +211,11 @@ def tile_cgblock_pb_k_kernel(
                 in_=planes.rearrange("p t (c i) -> p c t i", i=RUN),
             )
 
+        def open_gpsimd(r):
+            zero = small.tile([P, 1], F32)
+            nc.vector.memset(zero[:], 0.0)
+            zero_tiles[r] = zero
+
         def regroup_round(r):
             grouped = regrouped.tile([P, ROUND_COLS, PACK], BF16, align_bytes=64)
             grouped_tiles[r] = grouped
@@ -222,18 +228,18 @@ def tile_cgblock_pb_k_kernel(
                 out=grouped[:, SCALAR_COLS:, :],
                 in0=planes[:, :, SCALAR_COLS:].rearrange("p t c -> p c t"),
                 scalar1=1.0,
-                scalar2=0.0,
+                scalar2=zero_tiles[r][:],
                 op0=ALU.mult,
                 op1=ALU.add,
             )
 
-        def quantise_half(r, half):
-            if half == 0:
+        def quantise_part(r, part):
+            if part == 0:
                 codes = packed.tile([P, ROUND_COLS], U32, align_bytes=64)
                 scales = packed.tile([P, ROUND_COLS], U8, align_bytes=64)
                 packed_tiles[r] = (codes, scales)
             codes, scales = packed_tiles[r]
-            cols = slice(half * ROUND_COLS // 2, (half + 1) * ROUND_COLS // 2)
+            cols = slice(part * P, (part + 1) * P if part < 2 else ROUND_COLS)
             nc.vector.quantize_mx(
                 out=codes[:, cols].bitcast(FP8X4),
                 scales=scales[:, cols],
@@ -298,7 +304,9 @@ def tile_cgblock_pb_k_kernel(
         def live(r):
             return 0 <= r < ROUNDS
 
-        for step in range(ROUNDS + 4):
+        quantised_rounds = 0
+        finished = set()
+        for step in range(ROUNDS + 3):
             if live(step - 1):
                 std_round(step - 1)
             if live(step - 2):
@@ -306,22 +314,22 @@ def tile_cgblock_pb_k_kernel(
             ahead = step + 1
             if live(ahead):
                 transpose_round(ahead)
-            for unit in (3, 2, 1, 0, 7, 6, 5, 4):
+            quantised = [r for r in (step - 4, step - 3) if live(r) and step - r == (3 if r >= ROUNDS - 2 else 4)]
+            for unit in (3, 2, 1, 0):
                 if live(step):
                     stats_unit(step, unit)
                 if unit == 1 and live(step - 1):
                     affine_part(step - 1, 0)
-                if unit == 0 and live(step - 1):
-                    affine_part(step - 1, 1)
-                if unit == 7:
-                    if live(step - 3):
-                        quantise_half(step - 3, 0)
-                    if live(step - 1):
-                        affine_part(step - 1, 2)
-                    if live(step - 3):
-                        quantise_half(step - 3, 1)
-                    if live(step - 1):
-                        affine_part(step - 1, 3)
+            for part in range(3):
+                if live(step - 1):
+                    affine_part(step - 1, 1 + part)
+                if part == 2 and 0 <= step - 2 < ROUNDS - 2:
+                    open_gpsimd(step - 2)
+                for r in quantised:
+                    quantise_part(r, part)
+            for unit in (7, 6, 5, 4):
+                if live(step):
+                    stats_unit(step, unit)
             if live(step - 2):
                 regroup_round(step - 2)
             if step == 0:
@@ -330,9 +338,13 @@ def tile_cgblock_pb_k_kernel(
                         out=gain_shift[:, :, u, :],
                         in_=vectors_t[:, u, :].bitcast(BF16).rearrange("p (r e) -> p r e", e=2),
                     )
-            if live(step - 3):
-                multiply_round(step - 3)
-            if step - 4 >= 0 and (step - 4) % STREAM_ROUNDS == STREAM_ROUNDS - 1:
-                finish_stream((step - 4) // STREAM_ROUNDS)
+            for stream in range(STREAMS):
+                if quantised_rounds == STREAM_ROUNDS * (stream + 1) and stream not in finished:
+                    finish_stream(stream)
+                    finished.add(stream)
+            for r in quantised:
+                multiply_round(r)
+                quantised_rounds += 1
             if live(step - 1):
                 normalise_bank(step - 1, 0)
+        finish_stream(STREAMS - 1)

@@ -29,8 +29,7 @@ ROUND_UNITS = 2 * ROUND_GROUPS
 ROUND_FEATURES = ROUND_GROUPS * PACK
 STREAM_ROUNDS = GROUPS // ROUND_GROUPS
 ROUNDS = STREAMS * STREAM_ROUNDS
-CHUNK_GROUPS = 4
-CHUNK_ROUNDS = CHUNK_GROUPS // ROUND_GROUPS
+CHUNK_GROUPS = ROUND_GROUPS
 STREAM_CHUNKS = GROUPS // CHUNK_GROUPS
 CHUNKS = STREAMS * STREAM_CHUNKS
 X_BUFS = 8
@@ -64,10 +63,10 @@ def tile_cgblock_pb_k_kernel(
         x_pool = ctx.enter_context(tc.tile_pool(name="x", bufs=X_BUFS))
         small = ctx.enter_context(tc.tile_pool(name="small", bufs=3))
         hidden = ctx.enter_context(tc.tile_pool(name="hidden", bufs=3))
-        regrouped = ctx.enter_context(tc.tile_pool(name="regrouped", bufs=3))
+        regrouped = ctx.enter_context(tc.tile_pool(name="regrouped", bufs=2))
         packed = ctx.enter_context(tc.tile_pool(name="packed", bufs=2))
-        turned = ctx.enter_context(tc.psum_pool(name="turned", bufs=6))
-        sums = ctx.enter_context(tc.psum_pool(name="sums", bufs=2))
+        turned = ctx.enter_context(tc.psum_pool(name="turned", bufs=7))
+        sums = ctx.enter_context(tc.psum_pool(name="sums", bufs=1))
         ctx.enter_context(tc.manual_schedule())
 
         ident = const.tile([P, P], F32)
@@ -95,7 +94,7 @@ def tile_cgblock_pb_k_kernel(
         x_tiles = {}
         turned_tiles = {}
         stats_tiles = {}
-        std_tiles = {}
+        rstd_tiles = {}
         affine_tiles = {}
         plane_tiles = {}
         grouped_tiles = {}
@@ -126,106 +125,115 @@ def tile_cgblock_pb_k_kernel(
                 in_=w_words_dram[stream][groups].rearrange("g p n t -> p g (n t)").bitcast(I32),
             )
 
-        def transpose_round(r):
-            words = x_tiles[r // CHUNK_ROUNDS][:].bitcast(F32)
-            first = (r % CHUNK_ROUNDS) * ROUND_GROUPS
-            banks = []
-            for half in range(ROUND_GROUPS // BANK_GROUPS):
-                bank = turned.tile([P, BANK_UNITS, P], F32)
-                for j in range(BANK_UNITS):
-                    g = first + half * BANK_GROUPS + j // 2
-                    u = j % 2
-                    nc.tensor.transpose(
-                        bank[:, j, :], words[:, 2 * P * g + u : 2 * P * (g + 1) : 2], ident[:]
-                    )
-                banks.append(bank)
-            turned_tiles[r] = banks
-            chunk = r // CHUNK_ROUNDS + X_BUFS
-            if r % CHUNK_ROUNDS == CHUNK_ROUNDS - 1 and chunk < CHUNKS:
+        def transpose_bank(r, half):
+            words = x_tiles[r][:].bitcast(F32)
+            bank = turned.tile([P, BANK_UNITS, P], F32)
+            for j in range(BANK_UNITS):
+                g = half * BANK_GROUPS + j // 2
+                u = j % 2
+                nc.tensor.transpose(bank[:, j, :], words[:, 2 * P * g + u : 2 * P * (g + 1) : 2], ident[:])
+            turned_tiles[r, half] = bank
+            chunk = r + X_BUFS
+            if half == 1 and chunk < CHUNKS:
                 load_x(chunk)
                 if chunk < 2 * STREAM_CHUNKS:
                     load_weights(chunk)
 
-        def pairs_of(r, unit):
-            return turned_tiles[r][unit // BANK_UNITS][:, unit % BANK_UNITS, :].bitcast(BF16)
+        def pairs_of(r, half, j):
+            return turned_tiles[r, half][:, j, :].bitcast(BF16)
 
-        def stats_unit(r, unit):
-            if r not in stats_tiles:
-                stats = small.tile([P, ROUND_UNITS, 6], F32)
-                stats_tiles[r] = stats
-            nc.vector.bn_stats(out=stats_tiles[r][:, unit, :], in_=pairs_of(r, unit))
+        def batch_of(r):
+            if r < 2 or r >= ROUNDS - 2:
+                return (r,)
+            return (r - r % 2, r - r % 2 + 1)
 
-        def std_round(r):
-            by_feature = stats_tiles[r][:].rearrange("p n (e s) -> p (n e) s", s=3)
-            std = small.tile([P, ROUND_FEATURES], F32)
-            nc.scalar.activation(out=std[:], in_=by_feature[:, :, 2], func=ACT.Sqrt, bias=eps[:], scale=1.0 / P)
-            std_tiles[r] = std
+        def stats_bank(r, half):
+            batch = batch_of(r)
+            if batch not in stats_tiles:
+                stats = small.tile([P, len(batch) * ROUND_UNITS, 6], F32)
+                stats_tiles[batch] = stats
+            first = (r - batch[0]) * ROUND_UNITS + half * BANK_UNITS
+            for j in range(BANK_UNITS - 1, -1, -1):
+                nc.vector.bn_stats(out=stats_tiles[batch][:, first + j, :], in_=pairs_of(r, half, j))
 
-        def affine_part(r, part):
-            stream, q = divmod(r, STREAM_ROUNDS)
+        def rstd_batch(batch):
+            by_feature = stats_tiles[batch][:].rearrange("p n (e s) -> p (n e) s", s=3)
+            rstd = small.tile([P, len(batch) * ROUND_FEATURES], F32)
+            nc.scalar.activation(
+                out=rstd[:], in_=by_feature[:, :, 2], func=ACT.Abs_reciprocal_sqrt, bias=eps[:], scale=1.0 / P
+            )
+            rstd_tiles[batch] = rstd
+
+        def affine_part(batch, part):
+            stream, q = divmod(batch[0], STREAM_ROUNDS)
+            groups = len(batch) * ROUND_GROUPS
             gain_row = (2 * GROUPS if stream == 0 else 0) + q * ROUND_GROUPS
             shift_row = gain_row + GROUPS
-            gain = gain_shift[:, gain_row : gain_row + ROUND_GROUPS, :, :].rearrange("p g u e -> p (g u e)")
-            shift = gain_shift[:, shift_row : shift_row + ROUND_GROUPS, :, :].rearrange("p g u e -> p (g u e)")
-            mean = stats_tiles[r][:].rearrange("p n (e s) -> p (n e) s", s=3)[:, :, 1]
+            gain = gain_shift[:, gain_row : gain_row + groups, :, :].rearrange("p g u e -> p (g u e)")
+            shift = gain_shift[:, shift_row : shift_row + groups, :, :].rearrange("p g u e -> p (g u e)")
+            mean = stats_tiles[batch][:].rearrange("p n (e s) -> p (n e) s", s=3)[:, :, 1]
             if part == 0:
-                rstd = small.tile([P, ROUND_FEATURES], F32)
-                scale = small.tile([P, ROUND_FEATURES], F32)
-                moved = small.tile([P, ROUND_FEATURES], F32)
-                bias = small.tile([P, ROUND_FEATURES], F32)
-                affine_tiles[r] = (rstd, scale, moved, bias)
-            rstd, scale, moved, bias = affine_tiles[r]
+                scale = small.tile([P, len(batch) * ROUND_FEATURES], F32)
+                moved = small.tile([P, len(batch) * ROUND_FEATURES], F32)
+                bias = small.tile([P, len(batch) * ROUND_FEATURES], F32)
+                affine_tiles[batch] = (scale, moved, bias)
+            scale, moved, bias = affine_tiles[batch]
             if part == 0:
-                nc.vector.reciprocal(out=rstd[:], in_=std_tiles[r][:])
+                nc.vector.tensor_mul(out=scale[:], in0=rstd_tiles[batch][:], in1=gain)
             if part == 1:
-                nc.vector.tensor_mul(out=scale[:], in0=rstd[:], in1=gain)
-            if part == 2:
                 nc.vector.scalar_tensor_tensor(
                     out=moved[:], in0=mean, scalar=-1.0, in1=scale[:], op0=ALU.mult, op1=ALU.mult
                 )
-            if part == 3:
+            if part == 2:
                 nc.vector.tensor_add(out=bias[:], in0=moved[:], in1=shift)
 
         def normalise_bank(r, half):
-            rstd, scale, moved, bias = affine_tiles[r]
+            batch = batch_of(r)
+            scale, moved, bias = affine_tiles[batch]
             if half == 0:
                 planes = hidden.tile([P, PACK, ROUND_GROUPS, P], BF16)
                 plane_tiles[r] = planes
             planes = plane_tiles[r]
-            for unit in range(half * BANK_UNITS, (half + 1) * BANK_UNITS):
-                pairs = pairs_of(r, unit).rearrange("p (b e) -> p b e", e=2)
+            for j in range(BANK_UNITS):
+                pairs = pairs_of(r, half, j).rearrange("p (b e) -> p b e", e=2)
                 for e in range(2):
-                    f = 2 * unit + e
-                    nc.scalar.activation(
-                        out=planes[:, f % PACK, f // PACK, :],
-                        in_=pairs[:, :, e],
-                        func=ACT.Relu,
-                        bias=bias[:, f : f + 1],
-                        scale=scale[:, f : f + 1],
-                    )
+                    f = 2 * (half * BANK_UNITS + j) + e
+                    col = (r - batch[0]) * ROUND_FEATURES + f
+                    out = planes[:, f % PACK, f // PACK, :]
+                    scale_col = scale[:, col : col + 1]
+                    bias_col = bias[:, col : col + 1]
+                    if r == ROUNDS - 1:
+                        nc.vector.tensor_scalar(
+                            out=out,
+                            in0=pairs[:, :, e],
+                            scalar1=scale_col,
+                            scalar2=bias_col,
+                            op0=ALU.mult,
+                            op1=ALU.add,
+                        )
+                    else:
+                        nc.scalar.activation(
+                            out=out, in_=pairs[:, :, e], func=ACT.Relu, bias=bias_col, scale=scale_col
+                        )
 
-        def regroup_by_copy(r, cols, copy):
+        def columns_of(r, cols):
             planes = plane_tiles[r][:].rearrange("p t g b -> p t (g b)")[:, :, cols]
-            copy(
-                out=grouped_tiles[r][:, cols, :].rearrange("p (c i) t -> p c t i", i=RUN),
-                in_=planes.rearrange("p t (c i) -> p c t i", i=RUN),
+            words = grouped_tiles[r][:, cols, :]
+            return (
+                words.rearrange("p (c i) t -> p c t i", i=RUN),
+                planes.rearrange("p t (c i) -> p c t i", i=RUN),
             )
 
-        def open_gpsimd(r):
-            zero = small.tile([P, 1], F32)
-            nc.vector.memset(zero[:], 0.0)
-            zero_tiles[r] = zero
-
-        def regroup_round(r):
+        def regroup_on_scalar(r):
             grouped = regrouped.tile([P, ROUND_COLS, PACK], BF16, align_bytes=64)
             grouped_tiles[r] = grouped
-            if r >= ROUNDS - 2:
-                regroup_by_copy(r, slice(0, ROUND_COLS), nc.vector.tensor_copy)
-                return
-            regroup_by_copy(r, slice(0, SCALAR_COLS), nc.scalar.copy)
+            words, planes = columns_of(r, slice(0, SCALAR_COLS))
+            nc.scalar.copy(out=words, in_=planes)
+
+        def regroup_on_gpsimd(r):
             planes = plane_tiles[r][:].rearrange("p t g b -> p t (g b)")
             nc.gpsimd.tensor_scalar(
-                out=grouped[:, SCALAR_COLS:, :],
+                out=grouped_tiles[r][:, SCALAR_COLS:, :],
                 in0=planes[:, :, SCALAR_COLS:].rearrange("p t c -> p c t"),
                 scalar1=1.0,
                 scalar2=zero_tiles[r][:],
@@ -233,13 +241,23 @@ def tile_cgblock_pb_k_kernel(
                 op1=ALU.add,
             )
 
-        def quantise_part(r, part):
-            if part == 0:
+        def regroup_on_vector(r):
+            grouped = regrouped.tile([P, ROUND_COLS, PACK], BF16, align_bytes=64)
+            grouped_tiles[r] = grouped
+            words, planes = columns_of(r, slice(0, ROUND_COLS))
+            nc.vector.tensor_scalar(out=words, in0=planes, scalar1=0.0, scalar2=None, op0=ALU.max)
+
+        def open_gpsimd(r):
+            zero = small.tile([P, 1], F32)
+            nc.vector.memset(zero[:], 0.0)
+            zero_tiles[r] = zero
+
+        def quantise(r, cols):
+            if r not in packed_tiles:
                 codes = packed.tile([P, ROUND_COLS], U32, align_bytes=64)
                 scales = packed.tile([P, ROUND_COLS], U8, align_bytes=64)
                 packed_tiles[r] = (codes, scales)
             codes, scales = packed_tiles[r]
-            cols = slice(part * P, (part + 1) * P if part < 2 else ROUND_COLS)
             nc.vector.quantize_mx(
                 out=codes[:, cols].bitcast(FP8X4),
                 scales=scales[:, cols],
@@ -295,7 +313,8 @@ def tile_cgblock_pb_k_kernel(
         nc.sync.dma_start(out=c_bias[:], in_=c_b3.partition_broadcast(P))
         nc.sync.dma_start(out=s_bias[:], in_=s_b3.partition_broadcast(P))
 
-        transpose_round(0)
+        transpose_bank(0, 0)
+        transpose_bank(0, 1)
         vectors_t = turned.tile([P, BANK_UNITS, P], F32, tag="bank")
         gain_shift = const.tile([P, P, 2, 2], F32)
         for u in range(2):
@@ -304,47 +323,56 @@ def tile_cgblock_pb_k_kernel(
         def live(r):
             return 0 <= r < ROUNDS
 
-        quantised_rounds = 0
-        finished = set()
-        for step in range(ROUNDS + 3):
-            if live(step - 1):
-                std_round(step - 1)
-            if live(step - 2):
-                normalise_bank(step - 2, 1)
-            ahead = step + 1
-            if live(ahead):
-                transpose_round(ahead)
-            quantised = [r for r in (step - 4, step - 3) if live(r) and step - r == (3 if r >= ROUNDS - 2 else 4)]
-            for unit in (3, 2, 1, 0):
-                if live(step):
-                    stats_unit(step, unit)
-                if unit == 1 and live(step - 1):
-                    affine_part(step - 1, 0)
-            for part in range(3):
-                if live(step - 1):
-                    affine_part(step - 1, 1 + part)
-                if part == 2 and 0 <= step - 2 < ROUNDS - 2:
-                    open_gpsimd(step - 2)
-                for r in quantised:
-                    quantise_part(r, part)
-            for unit in (7, 6, 5, 4):
-                if live(step):
-                    stats_unit(step, unit)
-            if live(step - 2):
-                regroup_round(step - 2)
+        for step in range(ROUNDS + 1):
+            if live(step + 1):
+                transpose_bank(step + 1, 0)
+            done = step - 5
+            if done >= 0 and done % STREAM_ROUNDS == STREAM_ROUNDS - 1:
+                finish_stream(done // STREAM_ROUNDS)
+            if live(step):
+                stats_bank(step, 0)
+            batch = batch_of(step - 1) if step > 0 else ()
+            ends = step > 0 and batch[-1] == step - 1
+            pieces = (slice(0, P), slice(P, 2 * P), slice(2 * P, ROUND_COLS)) if ends else (slice(0, ROUND_COLS),)
+            for part, cols in enumerate(pieces):
+                if ends:
+                    affine_part(batch, part)
+                if part == len(pieces) - 1 and step >= 3:
+                    open_gpsimd(step - 3)
+                if step >= 4:
+                    quantise(step - 4, cols)
+            if live(step):
+                stats_bank(step, 1)
             if step == 0:
                 for u in range(2):
                     nc.vector.tensor_copy(
                         out=gain_shift[:, :, u, :],
                         in_=vectors_t[:, u, :].bitcast(BF16).rearrange("p (r e) -> p r e", e=2),
                     )
-            for stream in range(STREAMS):
-                if quantised_rounds == STREAM_ROUNDS * (stream + 1) and stream not in finished:
-                    finish_stream(stream)
-                    finished.add(stream)
-            for r in quantised:
-                multiply_round(r)
-                quantised_rounds += 1
-            if live(step - 1):
-                normalise_bank(step - 1, 0)
+            if step >= 3:
+                regroup_on_gpsimd(step - 3)
+            if step >= 4:
+                multiply_round(step - 4)
+            r = step - 1 if step < 3 else step - 2
+            normal = live(r) and step != 3
+            if normal:
+                normalise_bank(r, 0)
+            if live(step + 1):
+                transpose_bank(step + 1, 1)
+            if live(step) and batch_of(step)[-1] == step:
+                rstd_batch(batch_of(step))
+            if normal:
+                normalise_bank(r, 1)
+                if r < ROUNDS - 2:
+                    regroup_on_scalar(r)
+
+        normalise_bank(ROUNDS - 1, 0)
+        normalise_bank(ROUNDS - 1, 1)
+        quantise(ROUNDS - 3, slice(0, ROUND_COLS))
+        multiply_round(ROUNDS - 3)
+        for r in (ROUNDS - 2, ROUNDS - 1):
+            regroup_on_vector(r)
+        for r in (ROUNDS - 2, ROUNDS - 1):
+            quantise(r, slice(0, ROUND_COLS))
+            multiply_round(r)
         finish_stream(STREAMS - 1)

@@ -22,6 +22,8 @@ EPS = 1e-5
 
 GROUPS = D // K_PASS
 STREAMS = 1 + SLICES
+ORDER = (1, 2, 0, 3, 4)
+CONTEXT_TURN = ORDER.index(0)
 ROUND_GROUPS = 4
 BANK_GROUPS = 2
 BANK_UNITS = 2 * BANK_GROUPS
@@ -33,9 +35,12 @@ CHUNK_GROUPS = ROUND_GROUPS
 STREAM_CHUNKS = GROUPS // CHUNK_GROUPS
 CHUNKS = STREAMS * STREAM_CHUNKS
 X_BUFS = 8
+WEIGHT_LAG = 5
+CONTEXT_FIRST = STREAM_CHUNKS - 2
 RUN = 4
 ROUND_COLS = ROUND_GROUPS * P
-SCALAR_COLS = 3 * P // 4
+SCALAR_COLS = P
+TAIL_SCALAR_COLS = 5 * P // 2
 
 FLOPS = 2 * P * STREAMS * D * N
 
@@ -78,8 +83,8 @@ def tile_cgblock_pb_k_kernel(
         s_words = const.tile([P, GROUPS, N], U32, align_bytes=64)
         c_scales = const.tile([P, GROUPS, N], U8, align_bytes=64)
         s_scales = const.tile([P, GROUPS, N], U8, align_bytes=64)
-        nc.vector.memset(c_scales[:].bitcast(I32), 0)
         nc.vector.memset(s_scales[:].bitcast(I32), 0)
+        nc.gpsimd.memset(c_scales[:].bitcast(I32), 0)
         w_words = [c_words, s_words]
         w_scales = [c_scales, s_scales]
         w_words_dram = [c_w3_words, s_w3_words]
@@ -103,26 +108,31 @@ def tile_cgblock_pb_k_kernel(
         sum_tiles = {}
 
         def load_x(chunk):
-            stream, part = divmod(chunk, STREAM_CHUNKS)
+            turn, part = divmod(chunk, STREAM_CHUNKS)
+            stream = ORDER[turn]
             cols = slice(part * CHUNK_GROUPS * K_PASS, (part + 1) * CHUNK_GROUPS * K_PASS)
+            x_dram = c_z2[:, cols] if stream == 0 else s_z2[:, stream - 1, cols]
             x_sb = x_pool.tile([P, CHUNK_GROUPS * K_PASS], BF16)
-            nc.sync.dma_start(out=x_sb[:], in_=c_z2[:, cols] if stream == 0 else s_z2[:, stream - 1, cols])
+            pieces = ROUND_GROUPS // BANK_GROUPS if chunk == 0 else 1
+            width = CHUNK_GROUPS * K_PASS // pieces
+            for piece in range(pieces):
+                piece_cols = slice(piece * width, (piece + 1) * width)
+                nc.sync.dma_start(out=x_sb[:, piece_cols], in_=x_dram[:, piece_cols])
             x_tiles[chunk] = x_sb
 
-        def load_weights(chunk):
-            stream, part = divmod(chunk, STREAM_CHUNKS)
+        def load_weights(which, part):
             if part == 0:
                 for quad in range(4):
                     nc.sync.dma_start(
-                        out=w_scales[stream][32 * quad : 32 * quad + 4, :, :].bitcast(I32),
-                        in_=w_scales_dram[stream][:, 4 * quad : 4 * quad + 4, :]
+                        out=w_scales[which][32 * quad : 32 * quad + 4, :, :].bitcast(I32),
+                        in_=w_scales_dram[which][:, 4 * quad : 4 * quad + 4, :]
                         .rearrange("g r n -> r g n")
                         .bitcast(I32),
                     )
             groups = slice(part * CHUNK_GROUPS, (part + 1) * CHUNK_GROUPS)
             nc.sync.dma_start(
-                out=w_words[stream][:, groups, :].bitcast(I32),
-                in_=w_words_dram[stream][groups].rearrange("g p n t -> p g (n t)").bitcast(I32),
+                out=w_words[which][:, groups, :].bitcast(I32),
+                in_=w_words_dram[which][groups].rearrange("g p n t -> p g (n t)").bitcast(I32),
             )
 
         def transpose_bank(r, half):
@@ -136,8 +146,11 @@ def tile_cgblock_pb_k_kernel(
             chunk = r + X_BUFS
             if half == 1 and chunk < CHUNKS:
                 load_x(chunk)
-                if chunk < 2 * STREAM_CHUNKS:
-                    load_weights(chunk)
+                if chunk - WEIGHT_LAG < STREAM_CHUNKS:
+                    load_weights(1, chunk - WEIGHT_LAG)
+                part = r - CONTEXT_FIRST
+                if part >= 0 and part % 2 == 0 and part // 2 < STREAM_CHUNKS:
+                    load_weights(0, part // 2)
 
         def pairs_of(r, half, j):
             return turned_tiles[r, half][:, j, :].bitcast(BF16)
@@ -165,7 +178,8 @@ def tile_cgblock_pb_k_kernel(
             rstd_tiles[batch] = rstd
 
         def affine_part(batch, part):
-            stream, q = divmod(batch[0], STREAM_ROUNDS)
+            turn, q = divmod(batch[0], STREAM_ROUNDS)
+            stream = ORDER[turn]
             groups = len(batch) * ROUND_GROUPS
             gain_row = (2 * GROUPS if stream == 0 else 0) + q * ROUND_GROUPS
             shift_row = gain_row + GROUPS
@@ -224,10 +238,10 @@ def tile_cgblock_pb_k_kernel(
                 planes.rearrange("p t (c i) -> p c t i", i=RUN),
             )
 
-        def regroup_on_scalar(r):
+        def regroup_on_scalar(r, cols):
             grouped = regrouped.tile([P, ROUND_COLS, PACK], BF16, align_bytes=64)
             grouped_tiles[r] = grouped
-            words, planes = columns_of(r, slice(0, SCALAR_COLS))
+            words, planes = columns_of(r, slice(0, cols))
             nc.scalar.copy(out=words, in_=planes)
 
         def regroup_on_gpsimd(r):
@@ -241,10 +255,11 @@ def tile_cgblock_pb_k_kernel(
                 op1=ALU.add,
             )
 
-        def regroup_on_vector(r):
-            grouped = regrouped.tile([P, ROUND_COLS, PACK], BF16, align_bytes=64)
-            grouped_tiles[r] = grouped
-            words, planes = columns_of(r, slice(0, ROUND_COLS))
+        def regroup_on_vector(r, first):
+            if first == 0:
+                grouped = regrouped.tile([P, ROUND_COLS, PACK], BF16, align_bytes=64)
+                grouped_tiles[r] = grouped
+            words, planes = columns_of(r, slice(first, ROUND_COLS))
             nc.vector.tensor_scalar(out=words, in0=planes, scalar1=0.0, scalar2=None, op0=ALU.max)
 
         def open_gpsimd(r):
@@ -265,7 +280,8 @@ def tile_cgblock_pb_k_kernel(
             )
 
         def multiply_round(r):
-            stream, q = divmod(r, STREAM_ROUNDS)
+            turn, q = divmod(r, STREAM_ROUNDS)
+            stream = ORDER[turn]
             which = min(stream, 1)
             if q == 0:
                 acc = sums.tile([P, N], F32)
@@ -284,20 +300,27 @@ def tile_cgblock_pb_k_kernel(
                     stop=(g == GROUPS - 1),
                 )
 
-        def finish_stream(stream):
+        def gate(i, multiply):
+            multiply(out=s_out[:, i, :], in0=s_out[:, i, :], in1=c_out[:], op=ALU.mult)
+            nc.sync.dma_start(out=out_0[:, i, :], in_=s_out[:, i, :])
+
+        def finish_turn(turn):
+            stream = ORDER[turn]
             acc = sum_tiles[stream]
             if stream == 0:
                 nc.vector.tensor_add(out=c_out[:], in0=acc[:], in1=c_bias[:])
-                return
-            i = stream - 1
-            nc.vector.tensor_add(out=s_out[:, i, :], in0=acc[:], in1=s_bias[:])
-            nc.vector.tensor_mul(out=s_out[:, i, :], in0=s_out[:, i, :], in1=c_out[:])
-            nc.sync.dma_start(out=out_0[:, i, :], in_=s_out[:, i, :])
-            if i == 1:
-                nc.vector.tensor_max(out=pooled[:], in0=s_out[:, 0, :], in1=s_out[:, 1, :])
-            if i > 1:
-                nc.vector.tensor_max(out=pooled[:], in0=pooled[:], in1=s_out[:, i, :])
-            if i == SLICES - 1:
+            else:
+                nc.vector.tensor_add(out=s_out[:, stream - 1, :], in0=acc[:], in1=s_bias[:])
+            if turn == CONTEXT_TURN:
+                for earlier in ORDER[:turn]:
+                    gate(earlier - 1, nc.gpsimd.tensor_tensor)
+            elif CONTEXT_TURN < turn < STREAMS - 1:
+                gate(stream - 1, nc.gpsimd.tensor_tensor)
+                first, second = (earlier - 1 for earlier in ORDER[:CONTEXT_TURN])
+                nc.vector.tensor_max(out=pooled[:], in0=s_out[:, first, :], in1=s_out[:, second, :])
+            elif turn == STREAMS - 1:
+                gate(stream - 1, nc.vector.tensor_tensor)
+                nc.vector.tensor_max(out=pooled[:], in0=pooled[:], in1=s_out[:, stream - 1, :])
                 nc.scalar.dma_start(out=out_1[:], in_=pooled[:])
 
         load_x(0)
@@ -306,10 +329,10 @@ def tile_cgblock_pb_k_kernel(
             nc.sync.dma_start(
                 out=vectors[v * GROUPS : (v + 1) * GROUPS, :], in_=vector.rearrange("(g k) -> g k", k=K_PASS)
             )
-        load_weights(0)
         for chunk in range(1, X_BUFS):
             load_x(chunk)
-            load_weights(chunk)
+            if chunk >= WEIGHT_LAG:
+                load_weights(1, chunk - WEIGHT_LAG)
         nc.sync.dma_start(out=c_bias[:], in_=c_b3.partition_broadcast(P))
         nc.sync.dma_start(out=s_bias[:], in_=s_b3.partition_broadcast(P))
 
@@ -319,6 +342,11 @@ def tile_cgblock_pb_k_kernel(
         gain_shift = const.tile([P, P, 2, 2], F32)
         for u in range(2):
             nc.tensor.transpose(vectors_t[:, u, :], vectors[:].bitcast(F32)[:, u : 2 * P : 2], ident[:])
+        for u in range(2):
+            nc.scalar.copy(
+                out=gain_shift[:, :, u, :],
+                in_=vectors_t[:, u, :].bitcast(BF16).rearrange("p (r e) -> p r e", e=2),
+            )
 
         def live(r):
             return 0 <= r < ROUNDS
@@ -328,9 +356,12 @@ def tile_cgblock_pb_k_kernel(
                 transpose_bank(step + 1, 0)
             done = step - 5
             if done >= 0 and done % STREAM_ROUNDS == STREAM_ROUNDS - 1:
-                finish_stream(done // STREAM_ROUNDS)
+                finish_turn(done // STREAM_ROUNDS)
             if live(step):
                 stats_bank(step, 0)
+            if step == ROUNDS:
+                for stream in ORDER[CONTEXT_TURN + 1 : STREAMS - 1]:
+                    nc.vector.tensor_max(out=pooled[:], in0=pooled[:], in1=s_out[:, stream - 1, :])
             batch = batch_of(step - 1) if step > 0 else ()
             ends = step > 0 and batch[-1] == step - 1
             pieces = (slice(0, P), slice(P, 2 * P), slice(2 * P, ROUND_COLS)) if ends else (slice(0, ROUND_COLS),)
@@ -343,12 +374,6 @@ def tile_cgblock_pb_k_kernel(
                     quantise(step - 4, cols)
             if live(step):
                 stats_bank(step, 1)
-            if step == 0:
-                for u in range(2):
-                    nc.vector.tensor_copy(
-                        out=gain_shift[:, :, u, :],
-                        in_=vectors_t[:, u, :].bitcast(BF16).rearrange("p (r e) -> p r e", e=2),
-                    )
             if step >= 3:
                 regroup_on_gpsimd(step - 3)
             if step >= 4:
@@ -363,16 +388,15 @@ def tile_cgblock_pb_k_kernel(
                 rstd_batch(batch_of(step))
             if normal:
                 normalise_bank(r, 1)
-                if r < ROUNDS - 2:
-                    regroup_on_scalar(r)
+                regroup_on_scalar(r, SCALAR_COLS if r < ROUNDS - 2 else TAIL_SCALAR_COLS)
 
         normalise_bank(ROUNDS - 1, 0)
         normalise_bank(ROUNDS - 1, 1)
         quantise(ROUNDS - 3, slice(0, ROUND_COLS))
         multiply_round(ROUNDS - 3)
-        for r in (ROUNDS - 2, ROUNDS - 1):
-            regroup_on_vector(r)
+        regroup_on_vector(ROUNDS - 1, 0)
+        regroup_on_vector(ROUNDS - 2, TAIL_SCALAR_COLS)
         for r in (ROUNDS - 2, ROUNDS - 1):
             quantise(r, slice(0, ROUND_COLS))
             multiply_round(r)
-        finish_stream(STREAMS - 1)
+        finish_turn(STREAMS - 1)

from contextlib import ExitStack

import concourse.mybir as mybir
from concourse.masks import make_identity

F32 = mybir.dt.float32
BF16 = mybir.dt.bfloat16
I32 = mybir.dt.int32
U32 = mybir.dt.uint32
U8 = mybir.dt.uint8
FP8X4 = mybir.dt.float8_e4m3fn_x4
ACT = mybir.ActivationFunctionType
ALU = mybir.AluOpType

P = 128
PACK = 4
K_PASS = P * PACK
D = 16384
N = 256
SLICES = 4
EPS = 1e-5

GROUPS = D // K_PASS
STREAMS = 1 + SLICES
ORDER = (1, 2, 0, 3, 4)
CONTEXT_TURN = ORDER.index(0)
ROUND_GROUPS = 4
BANK_GROUPS = 2
BANK_UNITS = 2 * BANK_GROUPS
ROUND_UNITS = 2 * ROUND_GROUPS
ROUND_FEATURES = ROUND_GROUPS * PACK
STREAM_ROUNDS = GROUPS // ROUND_GROUPS
ROUNDS = STREAMS * STREAM_ROUNDS
CHUNK_GROUPS = ROUND_GROUPS
STREAM_CHUNKS = GROUPS // CHUNK_GROUPS
CHUNKS = STREAMS * STREAM_CHUNKS
X_BUFS = 8
WEIGHT_LAG = 5
CONTEXT_FIRST = STREAM_CHUNKS - 2
RUN = 4
ROUND_COLS = ROUND_GROUPS * P
SCALAR_COLS = P
TAIL_SCALAR_COLS = 5 * P // 2

FLOPS = 2 * P * STREAMS * D * N


def tile_cgblock_pb_k_kernel(
    tc,
    s_z2,
    c_z2,
    s_g2,
    s_be2,
    s_w3_words,
    s_w3_scales,
    s_b3,
    c_g2,
    c_be2,
    c_w3_words,
    c_w3_scales,
    c_b3,
    out_0,
    out_1,
):
    nc = tc.nc
    with ExitStack() as ctx:
        const = ctx.enter_context(tc.tile_pool(name="const", bufs=1))
        x_pool = ctx.enter_context(tc.tile_pool(name="x", bufs=X_BUFS))
        small = ctx.enter_context(tc.tile_pool(name="small", bufs=3))
        hidden = ctx.enter_context(tc.tile_pool(name="hidden", bufs=3))
        regrouped = ctx.enter_context(tc.tile_pool(name="regrouped", bufs=2))
        packed = ctx.enter_context(tc.tile_pool(name="packed", bufs=2))
        turned = ctx.enter_context(tc.psum_pool(name="turned", bufs=7))
        sums = ctx.enter_context(tc.psum_pool(name="sums", bufs=1))
        ctx.enter_context(tc.manual_schedule())

        ident = const.tile([P, P], F32)
        make_identity(nc, ident[:])
        eps = const.tile([P, 1], F32)
        nc.vector.memset(eps[:], EPS)

        c_words = const.tile([P, GROUPS, N], U32, align_bytes=64)
        s_words = const.tile([P, GROUPS, N], U32, align_bytes=64)
        c_scales = const.tile([P, GROUPS, N], U8, align_bytes=64)
        s_scales = const.tile([P, GROUPS, N], U8, align_bytes=64)
        nc.vector.memset(s_scales[:].bitcast(I32), 0)
        nc.gpsimd.memset(c_scales[:].bitcast(I32), 0)
        w_words = [c_words, s_words]
        w_scales = [c_scales, s_scales]
        w_words_dram = [c_w3_words, s_w3_words]
        w_scales_dram = [c_w3_scales, s_w3_scales]

        c_bias = const.tile([P, N], BF16)
        s_bias = const.tile([P, N], BF16)
        c_out = const.tile([P, N], F32)
        s_out = const.tile([P, SLICES, N], F32)
        pooled = const.tile([P, N], F32)

        x_tiles = {}
        turned_tiles = {}
        stats_tiles = {}
        rstd_tiles = {}
        affine_tiles = {}
        plane_tiles = {}
        grouped_tiles = {}
        zero_tiles = {}
        packed_tiles = {}
        sum_tiles = {}

        def load_x(chunk):
            turn, part = divmod(chunk, STREAM_CHUNKS)
            stream = ORDER[turn]
            cols = slice(part * CHUNK_GROUPS * K_PASS, (part + 1) * CHUNK_GROUPS * K_PASS)
            x_dram = c_z2[:, cols] if stream == 0 else s_z2[:, stream - 1, cols]
            x_sb = x_pool.tile([P, CHUNK_GROUPS * K_PASS], BF16)
            pieces = ROUND_GROUPS // BANK_GROUPS if chunk == 0 else 1
            width = CHUNK_GROUPS * K_PASS // pieces
            for piece in range(pieces):
                piece_cols = slice(piece * width, (piece + 1) * width)
                nc.sync.dma_start(out=x_sb[:, piece_cols], in_=x_dram[:, piece_cols])
            x_tiles[chunk] = x_sb

        def load_weights(which, part):
            if part == 0:
                for quad in range(4):
                    nc.sync.dma_start(
                        out=w_scales[which][32 * quad : 32 * quad + 4, :, :].bitcast(I32),
                        in_=w_scales_dram[which][:, 4 * quad : 4 * quad + 4, :]
                        .rearrange("g r n -> r g n")
                        .bitcast(I32),
                    )
            groups = slice(part * CHUNK_GROUPS, (part + 1) * CHUNK_GROUPS)
            nc.sync.dma_start(
                out=w_words[which][:, groups, :].bitcast(I32),
                in_=w_words_dram[which][groups].rearrange("g p n t -> p g (n t)").bitcast(I32),
            )

        def transpose_bank(r, half):
            words = x_tiles[r][:].bitcast(F32)
            bank = turned.tile([P, BANK_UNITS, P], F32)
            for j in range(BANK_UNITS):
                g = half * BANK_GROUPS + j // 2
                u = j % 2
                nc.tensor.transpose(bank[:, j, :], words[:, 2 * P * g + u : 2 * P * (g + 1) : 2], ident[:])
            turned_tiles[r, half] = bank
            chunk = r + X_BUFS
            if half == 1 and chunk < CHUNKS:
                load_x(chunk)
                if chunk - WEIGHT_LAG < STREAM_CHUNKS:
                    load_weights(1, chunk - WEIGHT_LAG)
                part = r - CONTEXT_FIRST
                if part >= 0 and part % 2 == 0 and part // 2 < STREAM_CHUNKS:
                    load_weights(0, part // 2)

        def pairs_of(r, half, j):
            return turned_tiles[r, half][:, j, :].bitcast(BF16)

        def batch_of(r):
            if r < 2 or r >= ROUNDS - 2:
                return (r,)
            return (r - r % 2, r - r % 2 + 1)

        def stats_bank(r, half):
            batch = batch_of(r)
            if batch not in stats_tiles:
                stats = small.tile([P, len(batch) * ROUND_UNITS, 6], F32)
                stats_tiles[batch] = stats
            first = (r - batch[0]) * ROUND_UNITS + half * BANK_UNITS
            for j in range(BANK_UNITS - 1, -1, -1):
                nc.vector.bn_stats(out=stats_tiles[batch][:, first + j, :], in_=pairs_of(r, half, j))

        def rstd_batch(batch):
            by_feature = stats_tiles[batch][:].rearrange("p n (e s) -> p (n e) s", s=3)
            rstd = small.tile([P, len(batch) * ROUND_FEATURES], F32)
            nc.scalar.activation(
                out=rstd[:], in_=by_feature[:, :, 2], func=ACT.Abs_reciprocal_sqrt, bias=eps[:], scale=1.0 / P
            )
            rstd_tiles[batch] = rstd

        def affine_part(batch, part):
            turn, q = divmod(batch[0], STREAM_ROUNDS)
            stream = ORDER[turn]
            groups = len(batch) * ROUND_GROUPS
            gain_row = (2 * GROUPS if stream == 0 else 0) + q * ROUND_GROUPS
            shift_row = gain_row + GROUPS
            gain = gain_shift[:, gain_row : gain_row + groups, :, :].rearrange("p g u e -> p (g u e)")
            shift = gain_shift[:, shift_row : shift_row + groups, :, :].rearrange("p g u e -> p (g u e)")
            mean = stats_tiles[batch][:].rearrange("p n (e s) -> p (n e) s", s=3)[:, :, 1]
            if part == 0:
                scale = small.tile([P, len(batch) * ROUND_FEATURES], F32)
                moved = small.tile([P, len(batch) * ROUND_FEATURES], F32)
                bias = small.tile([P, len(batch) * ROUND_FEATURES], F32)
                affine_tiles[batch] = (scale, moved, bias)
            scale, moved, bias = affine_tiles[batch]
            if part == 0:
                nc.vector.tensor_mul(out=scale[:], in0=rstd_tiles[batch][:], in1=gain)
            if part == 1:
                nc.vector.scalar_tensor_tensor(
                    out=moved[:], in0=mean, scalar=-1.0, in1=scale[:], op0=ALU.mult, op1=ALU.mult
                )
            if part == 2:
                nc.vector.tensor_add(out=bias[:], in0=moved[:], in1=shift)

        def normalise_bank(r, half):
            batch = batch_of(r)
            scale, moved, bias = affine_tiles[batch]
            if half == 0:
                planes = hidden.tile([P, PACK, ROUND_GROUPS, P], BF16)
                plane_tiles[r] = planes
            planes = plane_tiles[r]
            for j in range(BANK_UNITS):
                pairs = pairs_of(r, half, j).rearrange("p (b e) -> p b e", e=2)
                for e in range(2):
                    f = 2 * (half * BANK_UNITS + j) + e
                    col = (r - batch[0]) * ROUND_FEATURES + f
                    out = planes[:, f % PACK, f // PACK, :]
                    scale_col = scale[:, col : col + 1]
                    bias_col = bias[:, col : col + 1]
                    if r == ROUNDS - 1:
                        nc.vector.tensor_scalar(
                            out=out,
                            in0=pairs[:, :, e],
                            scalar1=scale_col,
                            scalar2=bias_col,
                            op0=ALU.mult,
                            op1=ALU.add,
                        )
                    else:
                        nc.scalar.activation(
                            out=out, in_=pairs[:, :, e], func=ACT.Relu, bias=bias_col, scale=scale_col
                        )

        def columns_of(r, cols):
            planes = plane_tiles[r][:].rearrange("p t g b -> p t (g b)")[:, :, cols]
            words = grouped_tiles[r][:, cols, :]
            return (
                words.rearrange("p (c i) t -> p c t i", i=RUN),
                planes.rearrange("p t (c i) -> p c t i", i=RUN),
            )

        def regroup_on_scalar(r, cols):
            grouped = regrouped.tile([P, ROUND_COLS, PACK], BF16, align_bytes=64)
            grouped_tiles[r] = grouped
            words, planes = columns_of(r, slice(0, cols))
            nc.scalar.copy(out=words, in_=planes)

        def regroup_on_gpsimd(r):
            planes = plane_tiles[r][:].rearrange("p t g b -> p t (g b)")
            nc.gpsimd.tensor_scalar(
                out=grouped_tiles[r][:, SCALAR_COLS:, :],
                in0=planes[:, :, SCALAR_COLS:].rearrange("p t c -> p c t"),
                scalar1=1.0,
                scalar2=zero_tiles[r][:],
                op0=ALU.mult,
                op1=ALU.add,
            )

        def regroup_on_vector(r, first):
            if first == 0:
                grouped = regrouped.tile([P, ROUND_COLS, PACK], BF16, align_bytes=64)
                grouped_tiles[r] = grouped
            words, planes = columns_of(r, slice(first, ROUND_COLS))
            nc.vector.tensor_scalar(out=words, in0=planes, scalar1=0.0, scalar2=None, op0=ALU.max)

        def open_gpsimd(r):
            zero = small.tile([P, 1], F32)
            nc.vector.memset(zero[:], 0.0)
            zero_tiles[r] = zero

        def quantise(r, cols):
            if r not in packed_tiles:
                codes = packed.tile([P, ROUND_COLS], U32, align_bytes=64)
                scales = packed.tile([P, ROUND_COLS], U8, align_bytes=64)
                packed_tiles[r] = (codes, scales)
            codes, scales = packed_tiles[r]
            nc.vector.quantize_mx(
                out=codes[:, cols].bitcast(FP8X4),
                scales=scales[:, cols],
                in_=grouped_tiles[r][:, cols, :].rearrange("p c t -> p (c t)"),
            )

        def multiply_round(r):
            turn, q = divmod(r, STREAM_ROUNDS)
            stream = ORDER[turn]
            which = min(stream, 1)
            if q == 0:
                acc = sums.tile([P, N], F32)
                sum_tiles[stream] = acc
            codes, scales = packed_tiles[r]
            for j in range(ROUND_GROUPS):
                g = q * ROUND_GROUPS + j
                rows = slice(j * P, (j + 1) * P)
                nc.tensor.matmul_mx(
                    out=sum_tiles[stream][:],
                    lhsT=codes[:, rows].bitcast(FP8X4),
                    lhsT_scale=scales[:, rows],
                    rhs=w_words[which][:, g, :].bitcast(FP8X4),
                    rhs_scale=w_scales[which][:, g, :],
                    start=(g == 0),
                    stop=(g == GROUPS - 1),
                )

        def gate(i, multiply):
            multiply(out=s_out[:, i, :], in0=s_out[:, i, :], in1=c_out[:], op=ALU.mult)
            nc.sync.dma_start(out=out_0[:, i, :], in_=s_out[:, i, :])

        def finish_turn(turn):
            stream = ORDER[turn]
            acc = sum_tiles[stream]
            if stream == 0:
                nc.vector.tensor_add(out=c_out[:], in0=acc[:], in1=c_bias[:])
            else:
                nc.vector.tensor_add(out=s_out[:, stream - 1, :], in0=acc[:], in1=s_bias[:])
            if turn == CONTEXT_TURN:
                for earlier in ORDER[:turn]:
                    gate(earlier - 1, nc.gpsimd.tensor_tensor)
            elif CONTEXT_TURN < turn < STREAMS - 1:
                gate(stream - 1, nc.gpsimd.tensor_tensor)
                first, second = (earlier - 1 for earlier in ORDER[:CONTEXT_TURN])
                nc.vector.tensor_max(out=pooled[:], in0=s_out[:, first, :], in1=s_out[:, second, :])
            elif turn == STREAMS - 1:
                gate(stream - 1, nc.vector.tensor_tensor)
                nc.vector.tensor_max(out=pooled[:], in0=pooled[:], in1=s_out[:, stream - 1, :])
                nc.scalar.dma_start(out=out_1[:], in_=pooled[:])

        load_x(0)
        vectors = const.tile([P, K_PASS], BF16)
        for v, vector in enumerate((s_g2, s_be2, c_g2, c_be2)):
            nc.sync.dma_start(
                out=vectors[v * GROUPS : (v + 1) * GROUPS, :], in_=vector.rearrange("(g k) -> g k", k=K_PASS)
            )
        for chunk in range(1, X_BUFS):
            load_x(chunk)
            if chunk >= WEIGHT_LAG:
                load_weights(1, chunk - WEIGHT_LAG)
        nc.sync.dma_start(out=c_bias[:], in_=c_b3.partition_broadcast(P))
        nc.sync.dma_start(out=s_bias[:], in_=s_b3.partition_broadcast(P))

        transpose_bank(0, 0)
        transpose_bank(0, 1)
        vectors_t = turned.tile([P, BANK_UNITS, P], F32, tag="bank")
        gain_shift = const.tile([P, P, 2, 2], F32)
        for u in range(2):
            nc.tensor.transpose(vectors_t[:, u, :], vectors[:].bitcast(F32)[:, u : 2 * P : 2], ident[:])
        for u in range(2):
            nc.scalar.copy(
                out=gain_shift[:, :, u, :],
                in_=vectors_t[:, u, :].bitcast(BF16).rearrange("p (r e) -> p r e", e=2),
            )

        def live(r):
            return 0 <= r < ROUNDS

        for step in range(ROUNDS + 1):
            if live(step + 1):
                transpose_bank(step + 1, 0)
            done = step - 5
            if done >= 0 and done % STREAM_ROUNDS == STREAM_ROUNDS - 1:
                finish_turn(done // STREAM_ROUNDS)
            if live(step):
                stats_bank(step, 0)
            if step == ROUNDS:
                for stream in ORDER[CONTEXT_TURN + 1 : STREAMS - 1]:
                    nc.vector.tensor_max(out=pooled[:], in0=pooled[:], in1=s_out[:, stream - 1, :])
            batch = batch_of(step - 1) if step > 0 else ()
            ends = step > 0 and batch[-1] == step - 1
            pieces = (slice(0, P), slice(P, 2 * P), slice(2 * P, ROUND_COLS)) if ends else (slice(0, ROUND_COLS),)
            for part, cols in enumerate(pieces):
                if ends:
                    affine_part(batch, part)
                if part == len(pieces) - 1 and step >= 3:
                    open_gpsimd(step - 3)
                if step >= 4:
                    quantise(step - 4, cols)
            if live(step):
                stats_bank(step, 1)
            if step >= 3:
                regroup_on_gpsimd(step - 3)
            if step >= 4:
                multiply_round(step - 4)
            r = step - 1 if step < 3 else step - 2
            normal = live(r) and step != 3
            if normal:
                normalise_bank(r, 0)
            if live(step + 1):
                transpose_bank(step + 1, 1)
            if live(step) and batch_of(step)[-1] == step:
                rstd_batch(batch_of(step))
            if normal:
                normalise_bank(r, 1)
                regroup_on_scalar(r, SCALAR_COLS if r < ROUNDS - 2 else TAIL_SCALAR_COLS)

        normalise_bank(ROUNDS - 1, 0)
        normalise_bank(ROUNDS - 1, 1)
        quantise(ROUNDS - 3, slice(0, ROUND_COLS))
        multiply_round(ROUNDS - 3)
        regroup_on_vector(ROUNDS - 1, 0)
        regroup_on_vector(ROUNDS - 2, TAIL_SCALAR_COLS)
        for r in (ROUNDS - 2, ROUNDS - 1):
            quantise(r, slice(0, ROUND_COLS))
            multiply_round(r)
        finish_turn(STREAMS - 1)
